import numpy as np
import ml_dtypes


def mxq(x, axis, fmt="e4m3"):
    dtype, down = {"e4m3": (ml_dtypes.float8_e4m3fn, 7), "e5m2": (ml_dtypes.float8_e5m2, 14)}[fmt]
    v = np.moveaxis(np.asarray(x, np.float32).astype(ml_dtypes.bfloat16).astype(np.float64), axis, -1)
    blocks = v.reshape(v.shape[:-1] + (-1, 32))
    amax = np.abs(blocks).max(-1, keepdims=True)
    byte = np.maximum(np.where(amax > 0, np.frexp(amax)[1] - 1 + 127, 0) - down, 1)
    scale = np.exp2(byte - 127.0)
    codes = (blocks / scale).astype(np.float32).astype(dtype).astype(np.float64)
    return np.moveaxis((codes * scale).reshape(v.shape), -1, axis)


WIDE = False


def mx_kscale(k):
    if not WIDE:
        return np.ones(k)
    levels = np.array([10, -10, 5, -5, 0])
    if k % 512:
        return np.exp2(np.random.permutation(np.resize(levels, k // 32))).repeat(32)
    a = np.empty((k // 512, 16))
    for p in range(k // 512):
        a[p, :8] = np.random.permutation(np.resize(levels, 8))
        for g in range(8):
            far = levels[np.abs(levels - a[p, g]) >= 10]
            a[p, g + 8] = far[np.random.randint(len(far))]
    return np.exp2(a.ravel()).repeat(32)


BF16 = ml_dtypes.bfloat16


def bf(x):
    return np.asarray(x, np.float32).astype(BF16)


def f64(x):
    return np.asarray(x).astype(np.float64)


B, L, D, C, S = 2, 64, 1024, 2, 8
EPS = 2.0 ** -23


def rmsnorm(h, w):
    return h / np.sqrt(np.mean(h * h, axis=-1, keepdims=True) + EPS) * w


def setup_inputs():
    s = mx_kscale(D)
    t = mx_kscale(C * D)
    tc = t.reshape(C, D, 1)
    n = np.random.standard_normal
    return {
        "x": bf(n((B, L, D)) * s),
        "real_state": bf(n((B, L, C, D, S)) * 0.5),
        "imag_state": bf(n((B, L, C, D, S)) * 0.5),
        "W_in": bf(n((C * D, D)) / np.sqrt(D) / s[None, :]),
        "A_theta": bf(n((C, D, S))),
        "B_real": bf(n((C, D, S)) * 0.5),
        "B_imag": bf(n((C, D, S)) * 0.5),
        "C_real": bf(n((C, D, S)) / np.sqrt(2 * S) * tc),
        "C_imag": bf(n((C, D, S)) / np.sqrt(2 * S) * tc),
        "W_out": bf(n((D, C * D)) / np.sqrt(C * D) / t[None, :]),
        "norm_w": bf((1.0 + 0.1 * n(D)) * s),
    }


def reference(x, real_state, imag_state, W_in, A_theta, B_real, B_imag, C_real, C_imag, W_out, norm_w):
    x = f64(x)
    rs, ims = f64(real_state), f64(imag_state)
    x_in = (mxq(x, 2, "e4m3") @ mxq(f64(W_in).T, 0, "e4m3")).reshape(B, L, C, D)[..., None]
    cos_t = np.cos(f64(A_theta))
    sin_t = np.sin(f64(A_theta))
    new_real = cos_t * rs - sin_t * ims + f64(B_real) * x_in
    new_imag = sin_t * rs + cos_t * ims + f64(B_imag) * x_in
    y = np.sum(f64(C_real) * new_real - f64(C_imag) * new_imag, axis=-1)
    out = mxq(y.reshape(B, L, C * D), 2, "e4m3") @ mxq(f64(W_out).T, 0, "e4m3")
    out = rmsnorm(out, f64(norm_w))
    return (x + out, new_real, new_imag)

@@ -1,0 +1,309 @@
+import math
+from contextlib import ExitStack
+
+import concourse.mybir as mybir
+from concourse.masks import make_identity
+
+F32 = mybir.dt.float32
+BF16 = mybir.dt.bfloat16
+U32 = mybir.dt.uint32
+U8 = mybir.dt.uint8
+FP8X4 = mybir.dt.float8_e4m3fn_x4
+ALU = mybir.AluOpType
+ACT = mybir.ActivationFunctionType
+
+P = 128
+D = 1024
+CD = 2048
+S = 8
+N_TILES = CD // P
+COLS = P * S
+PIECE = 4096
+PIECE_WORDS = PIECE // 4
+
+FLOPS = 2 * P * D * CD * 2
+
+EPS = 2.0 ** -23
+ROUND_MAGIC = 12582912.0
+TWO_PI_HI = 6.28125
+TWO_PI_MID = 0.0019353071693331003
+TWO_PI_LO = 2.0 * math.pi - TWO_PI_HI - TWO_PI_MID
+PI_BELOW = 3.1415925
+
+
+def load_coefficients(nc, pool, coeff, name):
+    raw = pool.tile([P, N_TILES * S], BF16, name=name)
+    nc.sync.dma_start(
+        out=raw[:].rearrange("p (k s) -> p k s", s=S),
+        in_=coeff.rearrange("c d s -> (c d) s").rearrange("(k p) s -> p k s", p=P))
+    return raw
+
+
+def transpose_word_blocks(nc, psum, ident_f32, rows_bf16):
+    words = rows_bf16.bitcast(F32)
+    bank = psum.tile([P, 4, P], F32, tag="out")
+    for b in range(4):
+        nc.tensor.transpose(bank[:, b, :], words[:, 256 * (b // 2) + b % 2 : 256 * (b // 2 + 1) : 2],
+                            ident_f32[:])
+    return bank
+
+
+def tile_recursivemamba130m_kernel(
+    tc, x, real_state, imag_state, W_in, A_theta, B_real, B_imag, C_real, C_imag, W_out, norm_w,
+    out_0, out_1, out_2,
+):
+    nc = tc.nc
+    with ExitStack() as ctx:
+        consts = ctx.enter_context(tc.tile_pool(name="consts", bufs=1))
+        tables = ctx.enter_context(tc.tile_pool(name="tables", bufs=1))
+        wstage = ctx.enter_context(tc.tile_pool(name="wstage", bufs=2))
+        wgroup = ctx.enter_context(tc.tile_pool(name="wgroup", bufs=2))
+        mxops = ctx.enter_context(tc.tile_pool(name="mxops", bufs=1))
+        mid = ctx.enter_context(tc.tile_pool(name="mid", bufs=1))
+        small = ctx.enter_context(tc.tile_pool(name="small", bufs=2))
+        stage = ctx.enter_context(tc.tile_pool(name="stage", bufs=3))
+        work = ctx.enter_context(tc.tile_pool(name="work", bufs=3))
+        leave = ctx.enter_context(tc.tile_pool(name="leave", bufs=3))
+        psum_in = ctx.enter_context(tc.psum_pool(name="psum_in", bufs=4))
+        psum_out = ctx.enter_context(tc.psum_pool(name="psum_out", bufs=4))
+
+        ident_f32 = consts.tile([P, P], F32)
+        make_identity(nc, ident_f32[:])
+
+        n_coef = N_TILES * S
+        theta = load_coefficients(nc, tables, A_theta, "theta")
+        turns = tables.tile([P, n_coef], F32)
+        nc.vector.tensor_scalar(out=turns[:], in0=theta[:], scalar1=1.0 / (2.0 * math.pi),
+                                scalar2=ROUND_MAGIC, op0=ALU.mult, op1=ALU.add)
+        nc.vector.tensor_scalar(out=turns[:], in0=turns[:], scalar1=ROUND_MAGIC, scalar2=None,
+                                op0=ALU.subtract)
+        reduced = tables.tile([P, n_coef], F32)
+        nc.vector.scalar_tensor_tensor(out=reduced[:], in0=turns[:], scalar=-TWO_PI_HI,
+                                       in1=theta[:], op0=ALU.mult, op1=ALU.add)
+        nc.vector.scalar_tensor_tensor(out=reduced[:], in0=turns[:], scalar=-TWO_PI_MID,
+                                       in1=reduced[:], op0=ALU.mult, op1=ALU.add)
+        nc.vector.scalar_tensor_tensor(out=reduced[:], in0=turns[:], scalar=-TWO_PI_LO,
+                                       in1=reduced[:], op0=ALU.mult, op1=ALU.add)
+        nc.vector.tensor_scalar(out=reduced[:], in0=reduced[:], scalar1=PI_BELOW,
+                                scalar2=-PI_BELOW, op0=ALU.min, op1=ALU.max)
+        sin_t = tables.tile([P, n_coef], F32)
+        nc.scalar.activation(out=sin_t[:], in_=reduced[:], func=ACT.Sin)
+        half = tables.tile([P, n_coef], F32)
+        nc.scalar.activation(out=half[:], in_=reduced[:], func=ACT.Sin, scale=0.5)
+        nc.scalar.activation(out=half[:], in_=half[:], func=ACT.Square, scale=math.sqrt(2.0))
+        cos_t = tables.tile([P, n_coef], F32)
+        nc.vector.tensor_scalar(out=cos_t[:], in0=half[:], scalar1=-1.0, scalar2=1.0,
+                                op0=ALU.mult, op1=ALU.add)
+        neg_sin_t = tables.tile([P, n_coef], F32)
+        nc.vector.tensor_scalar(out=neg_sin_t[:], in0=sin_t[:], scalar1=-1.0, scalar2=None,
+                                op0=ALU.mult)
+
+        x_sb = consts.tile([P, D], BF16)
+        nc.sync.dma_start(out=x_sb[:], in_=x.rearrange("b l d -> (b l) d"))
+        x_bank = transpose_word_blocks(nc, psum_out, ident_f32, x_sb[:])
+        x_grouped = mxops.tile([P, 2, P, 4], BF16, align_bytes=64)
+        nc.scalar.copy(out=x_grouped[:].bitcast(F32),
+                       in_=x_bank[:].rearrange("p (a u) n -> p a n u", u=2))
+        x_codes = mxops.tile([P, 2 * P], U32, align_bytes=64)
+        x_scales = mxops.tile([P, 2 * P], U8, align_bytes=64)
+        nc.vector.quantize_mx(out=x_codes[:].bitcast(FP8X4), scales=x_scales[:],
+                              in_=x_grouped[:].rearrange("p a n j -> p (a n j)"))
+
+        w_codes = mxops.tile([P, 4 * PIECE_WORDS], U32, align_bytes=64)
+        w_scales = mxops.tile([P, 4 * PIECE_WORDS], U8, align_bytes=64)
+        xin_t = mid.tile([P, N_TILES, P], F32)
+        for piece in range(4):
+            w_rows = wstage.tile([P, 4, D], BF16, tag="w_rows")
+            nc.sync.dma_start(
+                out=w_rows[:],
+                in_=W_in[piece * 512 : (piece + 1) * 512, :].rearrange("(r p) k -> p r k", p=P))
+            w_grouped = wgroup.tile([P, 2, 512, 4], BF16, tag="w_grouped", align_bytes=64)
+            for r in range(4):
+                w_bank = transpose_word_blocks(nc, psum_out, ident_f32, w_rows[:, r, :])
+                nc.scalar.copy(out=w_grouped[:, :, r * P : (r + 1) * P, :].bitcast(F32),
+                               in_=w_bank[:].rearrange("p (a u) n -> p a n u", u=2))
+            words = slice(piece * PIECE_WORDS, (piece + 1) * PIECE_WORDS)
+            nc.vector.quantize_mx(out=w_codes[:, words].bitcast(FP8X4), scales=w_scales[:, words],
+                                  in_=w_grouped[:].rearrange("p a n j -> p (a n j)"))
+            xin_bank = psum_in.tile([P, 4, P], F32, tag="in")
+            for r in range(4):
+                for a in range(2):
+                    cols = slice(piece * PIECE_WORDS + a * 512 + r * P,
+                                 piece * PIECE_WORDS + a * 512 + (r + 1) * P)
+                    nc.tensor.matmul_mx(out=xin_bank[:, r, :],
+                                        lhsT=w_codes[:, cols].bitcast(FP8X4),
+                                        lhsT_scale=w_scales[:, cols],
+                                        rhs=x_codes[:, a * P : (a + 1) * P].bitcast(FP8X4),
+                                        rhs_scale=x_scales[:, a * P : (a + 1) * P],
+                                        start=(a == 0), stop=(a == 1))
+            nc.scalar.copy(out=xin_t[:, piece * 4 : (piece + 1) * 4, :], in_=xin_bank[:])
+
+        b_raw = [load_coefficients(nc, tables, B_real, "b_real_raw"),
+                 load_coefficients(nc, tables, B_imag, "b_imag_raw")]
+        c_raw = [load_coefficients(nc, tables, C_real, "c_real_raw"),
+                 load_coefficients(nc, tables, C_imag, "c_imag_raw")]
+        b_real_t = tables.tile([P, n_coef], F32)
+        nc.vector.tensor_copy(out=b_real_t[:], in_=b_raw[0][:])
+        b_imag_t = tables.tile([P, n_coef], F32)
+        nc.vector.tensor_copy(out=b_imag_t[:], in_=b_raw[1][:])
+        c_real_t = tables.tile([P, n_coef], F32)
+        nc.vector.tensor_copy(out=c_real_t[:], in_=c_raw[0][:])
+        neg_c_imag_t = tables.tile([P, n_coef], F32)
+        nc.vector.tensor_scalar(out=neg_c_imag_t[:], in0=c_raw[1][:], scalar1=-1.0, scalar2=None,
+                                op0=ALU.mult)
+        norm_w_all = consts.tile([P, D], BF16)
+        nc.sync.dma_start(out=norm_w_all[:], in_=norm_w.partition_broadcast(P))
+
+        wo_codes = mxops.tile([P, 4 * PIECE_WORDS], U32, align_bytes=64)
+        wo_scales = mxops.tile([P, 4 * PIECE_WORDS], U8, align_bytes=64)
+
+        def prepare_w_out(piece):
+            wo_rows = wstage.tile([P, 2, CD], BF16, tag="w_rows")
+            nc.sync.dma_start(
+                out=wo_rows[:],
+                in_=W_out[piece * 256 : (piece + 1) * 256, :].rearrange("(r p) k -> p r k", p=P))
+            wo_grouped = wgroup.tile([P, 4, 256, 4], BF16, tag="w_grouped", align_bytes=64)
+            for r in range(2):
+                for half_k in range(2):
+                    wo_bank = transpose_word_blocks(
+                        nc, psum_out, ident_f32, wo_rows[:, r, half_k * D : (half_k + 1) * D])
+                    nc.scalar.copy(
+                        out=wo_grouped[:, half_k * 2 : (half_k + 1) * 2,
+                                       r * P : (r + 1) * P, :].bitcast(F32),
+                        in_=wo_bank[:].rearrange("p (a u) n -> p a n u", u=2))
+            words = slice(piece * PIECE_WORDS, (piece + 1) * PIECE_WORDS)
+            nc.vector.quantize_mx(out=wo_codes[:, words].bitcast(FP8X4),
+                                  scales=wo_scales[:, words],
+                                  in_=wo_grouped[:].rearrange("p c n q -> p (c n q)"))
+
+        state_in = [real_state.rearrange("b l c d s -> (b l) (c d s)"),
+                    imag_state.rearrange("b l c d s -> (b l) (c d s)")]
+        state_out = [out_1.rearrange("b l c d s -> (b l) (c d s)"),
+                     out_2.rearrange("b l c d s -> (b l) (c d s)")]
+        y_t = mid.tile([P, N_TILES, P], F32)
+        y_grouped = mxops.tile([P, 4, P, 4], BF16, align_bytes=64)
+        y_codes = mxops.tile([P, 4 * P], U32, align_bytes=64)
+        y_scales = mxops.tile([P, 4 * P], U8, align_bytes=64)
+        for k in range(N_TILES):
+            cols = slice(k * COLS, (k + 1) * COLS)
+            old_t = []
+            for h in range(2):
+                rows = stage.tile([P, COLS], BF16, tag="rows%d" % h)
+                nc.sync.dma_start(out=rows[:], in_=state_in[h][:, cols])
+                words = rows[:].bitcast(F32).rearrange("t (f q) -> t q f", q=4)
+                bank = psum_in.tile([P, 4, P], F32, tag="in")
+                for q in range(4):
+                    nc.tensor.transpose(bank[:, q, :], words[:, q, :], ident_f32[:])
+                old_t.append(bank[:].bitcast(BF16).rearrange("p q (t e) -> p q e t", e=2))
+            old_real_t, old_imag_t = old_t
+
+            new_real_t = work.tile([P, S, P], F32, tag="new_real_t")
+            new_imag_t = work.tile([P, S, P], F32, tag="new_imag_t")
+            for s in range(S):
+                one = slice(k * S + s, k * S + s + 1)
+                nc.scalar.activation(out=new_real_t[:, s, :], in_=old_real_t[:, s // 2, s % 2, :],
+                                     func=ACT.Copy, scale=cos_t[:, one])
+                nc.scalar.activation(out=new_imag_t[:, s, :], in_=old_real_t[:, s // 2, s % 2, :],
+                                     func=ACT.Copy, scale=sin_t[:, one])
+            for s in range(S):
+                one = slice(k * S + s, k * S + s + 1)
+                nc.vector.scalar_tensor_tensor(
+                    out=new_real_t[:, s, :], in0=old_imag_t[:, s // 2, s % 2, :],
+                    scalar=neg_sin_t[:, one], in1=new_real_t[:, s, :], op0=ALU.mult, op1=ALU.add)
+                nc.vector.scalar_tensor_tensor(
+                    out=new_imag_t[:, s, :], in0=old_imag_t[:, s // 2, s % 2, :],
+                    scalar=cos_t[:, one], in1=new_imag_t[:, s, :], op0=ALU.mult, op1=ALU.add)
+            for s in range(S):
+                one = slice(k * S + s, k * S + s + 1)
+                nc.vector.scalar_tensor_tensor(
+                    out=new_real_t[:, s, :], in0=xin_t[:, k, :], scalar=b_real_t[:, one],
+                    in1=new_real_t[:, s, :], op0=ALU.mult, op1=ALU.add)
+                nc.vector.scalar_tensor_tensor(
+                    out=new_imag_t[:, s, :], in0=xin_t[:, k, :], scalar=b_imag_t[:, one],
+                    in1=new_imag_t[:, s, :], op0=ALU.mult, op1=ALU.add)
+
+            for h, new_t in enumerate((new_real_t, new_imag_t)):
+                new_rows = leave.tile([P, P, S], F32, tag="new_rows%d" % h)
+                for half_s in range(2):
+                    back = psum_out.tile([P, 4, P], F32, tag="out")
+                    for j in range(4):
+                        nc.tensor.transpose(back[:, j, :], new_t[:, half_s * 4 + j, :], ident_f32[:])
+                    nc.scalar.copy(out=new_rows[:, :, half_s * 4 : (half_s + 1) * 4],
+                                   in_=back[:].rearrange("t j f -> t f j"))
+                nc.sync.dma_start(out=state_out[h][:, cols],
+                                  in_=new_rows[:].rearrange("t f s -> t (f s)"))
+
+            y_imag_part = small.tile([P, P], F32, tag="y_imag_part")
+            for s in range(S):
+                one = slice(k * S + s, k * S + s + 1)
+                if s == 0:
+                    nc.vector.tensor_scalar(out=y_t[:, k, :], in0=new_real_t[:, s, :],
+                                            scalar1=c_real_t[:, one], scalar2=None, op0=ALU.mult)
+                    nc.vector.tensor_scalar(out=y_imag_part[:], in0=new_imag_t[:, s, :],
+                                            scalar1=neg_c_imag_t[:, one], scalar2=None, op0=ALU.mult)
+                else:
+                    nc.vector.scalar_tensor_tensor(
+                        out=y_t[:, k, :], in0=new_real_t[:, s, :], scalar=c_real_t[:, one],
+                        in1=y_t[:, k, :], op0=ALU.mult, op1=ALU.add)
+                    nc.vector.scalar_tensor_tensor(
+                        out=y_imag_part[:], in0=new_imag_t[:, s, :], scalar=neg_c_imag_t[:, one],
+                        in1=y_imag_part[:], op0=ALU.mult, op1=ALU.add)
+            nc.vector.tensor_tensor(out=y_t[:, k, :], in0=y_t[:, k, :], in1=y_imag_part[:], op=ALU.add)
+
+            if k % 4 == 3:
+                c = k // 4
+                y_back = psum_out.tile([P, 4, P], F32, tag="out")
+                for q in range(4):
+                    nc.tensor.transpose(y_back[:, q, :], y_t[:, c * 4 + q, :], ident_f32[:])
+                y_rows = small.tile([P, 512], BF16, tag="y_rows")
+                nc.scalar.copy(out=y_rows[:], in_=y_back[:].rearrange("t q f -> t (q f)"))
+                y_words = y_rows[:].bitcast(F32)
+                y_bank = psum_out.tile([P, 2, P], F32, tag="out")
+                for u in range(2):
+                    nc.tensor.transpose(y_bank[:, u, :], y_words[:, u : 256 : 2], ident_f32[:])
+                nc.scalar.copy(out=y_grouped[:, c, :, :].bitcast(F32),
+                               in_=y_bank[:].rearrange("p u t -> p t u"))
+                nc.vector.quantize_mx(out=y_codes[:, c * P : (c + 1) * P].bitcast(FP8X4),
+                                      scales=y_scales[:, c * P : (c + 1) * P],
+                                      in_=y_grouped[:, c, :, :].rearrange("p t q -> p (t q)"))
+            if k % 4 == 1:
+                prepare_w_out(k // 4)
+
+        o_banks = []
+        for nb in range(2):
+            o_bank = psum_in.tile([P, 2, 256], F32, tag="in")
+            o_banks.append(o_bank)
+            for i in range(2):
+                piece = nb * 2 + i
+                for c in range(4):
+                    cols = slice(piece * PIECE_WORDS + c * 256, piece * PIECE_WORDS + (c + 1) * 256)
+                    nc.tensor.matmul_mx(out=o_bank[:, i, :],
+                                        lhsT=y_codes[:, c * P : (c + 1) * P].bitcast(FP8X4),
+                                        lhsT_scale=y_scales[:, c * P : (c + 1) * P],
+                                        rhs=wo_codes[:, cols].bitcast(FP8X4),
+                                        rhs_scale=wo_scales[:, cols],
+                                        start=(c == 0), stop=(c == 3))
+
+        sums = small.tile([P, 2], F32)
+        for nb in range(2):
+            squares = small.tile([P, 512], F32, tag="squares")
+            nc.scalar.activation(out=squares[:], in_=o_banks[nb][:].rearrange("p i n -> p (i n)"),
+                                 func=ACT.Square, accum_out=sums[:, nb : nb + 1])
+        mean_sq = small.tile([P, 1], F32)
+        nc.vector.tensor_tensor(out=mean_sq[:], in0=sums[:, 0:1], in1=sums[:, 1:2], op=ALU.add)
+        nc.vector.tensor_scalar(out=mean_sq[:], in0=mean_sq[:], scalar1=1.0 / D, scalar2=EPS,
+                                op0=ALU.mult, op1=ALU.add)
+        rms = small.tile([P, 1], F32)
+        nc.scalar.activation(out=rms[:], in_=mean_sq[:], func=ACT.Sqrt)
+        inv_rms = small.tile([P, 1], F32)
+        nc.vector.reciprocal(out=inv_rms[:], in_=rms[:])
+        result = mid.tile([P, D], F32)
+        for nb in range(2):
+            cols = slice(nb * 512, (nb + 1) * 512)
+            nc.vector.scalar_tensor_tensor(out=result[:, cols],
+                                           in0=o_banks[nb][:].rearrange("p i n -> p (i n)"),
+                                           scalar=inv_rms[:, 0:1], in1=norm_w_all[:, cols],
+                                           op0=ALU.mult, op1=ALU.mult)
+            nc.vector.tensor_tensor(out=result[:, cols], in0=result[:, cols], in1=x_sb[:, cols],
+                                    op=ALU.add)
+        nc.sync.dma_start(out=out_0.rearrange("b l d -> (b l) d"), in_=result[:])

@@ -11,6 +11,7 @@ U8 = mybir.dt.uint8
 FP8X4 = mybir.dt.float8_e4m3fn_x4
 ALU = mybir.AluOpType
 ACT = mybir.ActivationFunctionType
+AX = mybir.AxisListType
 
 P = 128
 D = 1024
@@ -18,8 +19,6 @@ CD = 2048
 S = 8
 N_TILES = CD // P
 COLS = P * S
-PIECE = 4096
-PIECE_WORDS = PIECE // 4
 
 FLOPS = 2 * P * D * CD * 2
 
@@ -56,12 +55,12 @@ def tile_recursivemamba130m_kernel(
     with ExitStack() as ctx:
         consts = ctx.enter_context(tc.tile_pool(name="consts", bufs=1))
         tables = ctx.enter_context(tc.tile_pool(name="tables", bufs=1))
-        wstage = ctx.enter_context(tc.tile_pool(name="wstage", bufs=2))
-        wgroup = ctx.enter_context(tc.tile_pool(name="wgroup", bufs=2))
+        wstage = ctx.enter_context(tc.tile_pool(name="wstage", bufs=4))
+        wgroup = ctx.enter_context(tc.tile_pool(name="wgroup", bufs=3))
         mxops = ctx.enter_context(tc.tile_pool(name="mxops", bufs=1))
         mid = ctx.enter_context(tc.tile_pool(name="mid", bufs=1))
         small = ctx.enter_context(tc.tile_pool(name="small", bufs=2))
-        stage = ctx.enter_context(tc.tile_pool(name="stage", bufs=3))
+        stage = ctx.enter_context(tc.tile_pool(name="stage", bufs=6))
         work = ctx.enter_context(tc.tile_pool(name="work", bufs=3))
         leave = ctx.enter_context(tc.tile_pool(name="leave", bufs=3))
         psum_in = ctx.enter_context(tc.psum_pool(name="psum_in", bufs=4))
@@ -70,8 +69,34 @@ def tile_recursivemamba130m_kernel(
         ident_f32 = consts.tile([P, P], F32)
         make_identity(nc, ident_f32[:])
 
-        n_coef = N_TILES * S
+        state_in = [real_state.rearrange("b l c d s -> (b l) (c d s)"),
+                    imag_state.rearrange("b l c d s -> (b l) (c d s)")]
+        state_out = [out_1.rearrange("b l c d s -> (b l) (c d s)"),
+                     out_2.rearrange("b l c d s -> (b l) (c d s)")]
+
         theta = load_coefficients(nc, tables, A_theta, "theta")
+        x_sb = consts.tile([P, D], BF16)
+        nc.sync.dma_start(out=x_sb[:], in_=x.rearrange("b l d -> (b l) d"))
+
+        def load_state(k):
+            both = []
+            for h in range(2):
+                rows = stage.tile([P, COLS], BF16, tag="rows%d" % h)
+                nc.sync.dma_start(out=rows[:], in_=state_in[h][:, k * COLS : (k + 1) * COLS])
+                both.append(rows)
+            return both
+
+        def load_w_in(k):
+            rows = wstage.tile([P, D], BF16, tag="w_in_rows")
+            nc.sync.dma_start(out=rows[:], in_=W_in[k * P : (k + 1) * P, :])
+            return rows
+
+        def load_w_out(r):
+            rows = wstage.tile([P, CD], BF16, tag="w_out_rows")
+            nc.sync.dma_start(out=rows[:], in_=W_out[r * P : (r + 1) * P, :])
+            return rows
+
+        n_coef = N_TILES * S
         turns = tables.tile([P, n_coef], F32)
         nc.vector.tensor_scalar(out=turns[:], in0=theta[:], scalar1=1.0 / (2.0 * math.pi),
                                 scalar2=ROUND_MAGIC, op0=ALU.mult, op1=ALU.add)
@@ -98,8 +123,6 @@ def tile_recursivemamba130m_kernel(
         nc.vector.tensor_scalar(out=neg_sin_t[:], in0=sin_t[:], scalar1=-1.0, scalar2=None,
                                 op0=ALU.mult)
 
-        x_sb = consts.tile([P, D], BF16)
-        nc.sync.dma_start(out=x_sb[:], in_=x.rearrange("b l d -> (b l) d"))
         x_bank = transpose_word_blocks(nc, psum_out, ident_f32, x_sb[:])
         x_grouped = mxops.tile([P, 2, P, 4], BF16, align_bytes=64)
         nc.scalar.copy(out=x_grouped[:].bitcast(F32),
@@ -109,179 +132,215 @@ def tile_recursivemamba130m_kernel(
         nc.vector.quantize_mx(out=x_codes[:].bitcast(FP8X4), scales=x_scales[:],
                               in_=x_grouped[:].rearrange("p a n j -> p (a n j)"))
 
-        w_codes = mxops.tile([P, 4 * PIECE_WORDS], U32, align_bytes=64)
-        w_scales = mxops.tile([P, 4 * PIECE_WORDS], U8, align_bytes=64)
         xin_t = mid.tile([P, N_TILES, P], F32)
-        for piece in range(4):
-            w_rows = wstage.tile([P, 4, D], BF16, tag="w_rows")
-            nc.sync.dma_start(
-                out=w_rows[:],
-                in_=W_in[piece * 512 : (piece + 1) * 512, :].rearrange("(r p) k -> p r k", p=P))
-            w_grouped = wgroup.tile([P, 2, 512, 4], BF16, tag="w_grouped", align_bytes=64)
-            for r in range(4):
-                w_bank = transpose_word_blocks(nc, psum_out, ident_f32, w_rows[:, r, :])
-                nc.scalar.copy(out=w_grouped[:, :, r * P : (r + 1) * P, :].bitcast(F32),
-                               in_=w_bank[:].rearrange("p (a u) n -> p a n u", u=2))
-            words = slice(piece * PIECE_WORDS, (piece + 1) * PIECE_WORDS)
-            nc.vector.quantize_mx(out=w_codes[:, words].bitcast(FP8X4), scales=w_scales[:, words],
+
+        def make_x_in(k, w_rows):
+            w_bank = transpose_word_blocks(nc, psum_out, ident_f32, w_rows[:])
+            w_grouped = wgroup.tile([P, 2, P, 4], BF16, tag="w_in_grouped", align_bytes=64)
+            nc.scalar.copy(out=w_grouped[:].bitcast(F32),
+                           in_=w_bank[:].rearrange("p (a u) n -> p a n u", u=2))
+            codes = wgroup.tile([P, 2 * P], U32, tag="w_in_codes", align_bytes=64)
+            scales = wgroup.tile([P, 2 * P], U8, tag="w_in_scales", align_bytes=64)
+            nc.vector.quantize_mx(out=codes[:].bitcast(FP8X4), scales=scales[:],
                                   in_=w_grouped[:].rearrange("p a n j -> p (a n j)"))
-            xin_bank = psum_in.tile([P, 4, P], F32, tag="in")
-            for r in range(4):
-                for a in range(2):
-                    cols = slice(piece * PIECE_WORDS + a * 512 + r * P,
-                                 piece * PIECE_WORDS + a * 512 + (r + 1) * P)
-                    nc.tensor.matmul_mx(out=xin_bank[:, r, :],
-                                        lhsT=w_codes[:, cols].bitcast(FP8X4),
-                                        lhsT_scale=w_scales[:, cols],
-                                        rhs=x_codes[:, a * P : (a + 1) * P].bitcast(FP8X4),
-                                        rhs_scale=x_scales[:, a * P : (a + 1) * P],
-                                        start=(a == 0), stop=(a == 1))
-            nc.scalar.copy(out=xin_t[:, piece * 4 : (piece + 1) * 4, :], in_=xin_bank[:])
+            xin_bank = psum_out.tile([P, P], F32, tag="out")
+            for a in range(2):
+                cols = slice(a * P, (a + 1) * P)
+                nc.tensor.matmul_mx(out=xin_bank[:], lhsT=codes[:, cols].bitcast(FP8X4),
+                                    lhsT_scale=scales[:, cols],
+                                    rhs=x_codes[:, cols].bitcast(FP8X4), rhs_scale=x_scales[:, cols],
+                                    start=(a == 0), stop=(a == 1))
+            nc.scalar.copy(out=xin_t[:, k, :], in_=xin_bank[:])
 
-        b_raw = [load_coefficients(nc, tables, B_real, "b_real_raw"),
-                 load_coefficients(nc, tables, B_imag, "b_imag_raw")]
-        c_raw = [load_coefficients(nc, tables, C_real, "c_real_raw"),
-                 load_coefficients(nc, tables, C_imag, "c_imag_raw")]
-        b_real_t = tables.tile([P, n_coef], F32)
-        nc.vector.tensor_copy(out=b_real_t[:], in_=b_raw[0][:])
-        b_imag_t = tables.tile([P, n_coef], F32)
-        nc.vector.tensor_copy(out=b_imag_t[:], in_=b_raw[1][:])
-        c_real_t = tables.tile([P, n_coef], F32)
-        nc.vector.tensor_copy(out=c_real_t[:], in_=c_raw[0][:])
-        neg_c_imag_t = tables.tile([P, n_coef], F32)
-        nc.vector.tensor_scalar(out=neg_c_imag_t[:], in0=c_raw[1][:], scalar1=-1.0, scalar2=None,
-                                op0=ALU.mult)
-        norm_w_all = consts.tile([P, D], BF16)
-        nc.sync.dma_start(out=norm_w_all[:], in_=norm_w.partition_broadcast(P))
+        wo_codes = mxops.tile([P, 8, 4 * P], U32, align_bytes=64)
+        wo_scales = mxops.tile([P, 8, 4 * P], U8, align_bytes=64)
 
-        wo_codes = mxops.tile([P, 4 * PIECE_WORDS], U32, align_bytes=64)
-        wo_scales = mxops.tile([P, 4 * PIECE_WORDS], U8, align_bytes=64)
-
-        def prepare_w_out(piece):
-            wo_rows = wstage.tile([P, 2, CD], BF16, tag="w_rows")
-            nc.sync.dma_start(
-                out=wo_rows[:],
-                in_=W_out[piece * 256 : (piece + 1) * 256, :].rearrange("(r p) k -> p r k", p=P))
-            wo_grouped = wgroup.tile([P, 4, 256, 4], BF16, tag="w_grouped", align_bytes=64)
-            for r in range(2):
-                for half_k in range(2):
-                    wo_bank = transpose_word_blocks(
-                        nc, psum_out, ident_f32, wo_rows[:, r, half_k * D : (half_k + 1) * D])
-                    nc.scalar.copy(
-                        out=wo_grouped[:, half_k * 2 : (half_k + 1) * 2,
-                                       r * P : (r + 1) * P, :].bitcast(F32),
-                        in_=wo_bank[:].rearrange("p (a u) n -> p a n u", u=2))
-            words = slice(piece * PIECE_WORDS, (piece + 1) * PIECE_WORDS)
-            nc.vector.quantize_mx(out=wo_codes[:, words].bitcast(FP8X4),
-                                  scales=wo_scales[:, words],
+        def prepare_w_out(r, half_k, wo_rows):
+            wo_bank = transpose_word_blocks(nc, psum_out, ident_f32,
+                                            wo_rows[:, half_k * D : (half_k + 1) * D])
+            wo_grouped = wgroup.tile([P, 2, P, 4], BF16, tag="w_out_grouped", align_bytes=64)
+            nc.vector.tensor_copy(out=wo_grouped[:].bitcast(F32),
+                                  in_=wo_bank[:].rearrange("p (a u) n -> p a n u", u=2))
+            words = slice(half_k * 2 * P, (half_k + 1) * 2 * P)
+            nc.vector.quantize_mx(out=wo_codes[:, r, words].bitcast(FP8X4),
+                                  scales=wo_scales[:, r, words],
                                   in_=wo_grouped[:].rearrange("p c n q -> p (c n q)"))
 
-        state_in = [real_state.rearrange("b l c d s -> (b l) (c d s)"),
-                    imag_state.rearrange("b l c d s -> (b l) (c d s)")]
-        state_out = [out_1.rearrange("b l c d s -> (b l) (c d s)"),
-                     out_2.rearrange("b l c d s -> (b l) (c d s)")]
-        y_t = mid.tile([P, N_TILES, P], F32)
         y_grouped = mxops.tile([P, 4, P, 4], BF16, align_bytes=64)
         y_codes = mxops.tile([P, 4 * P], U32, align_bytes=64)
         y_scales = mxops.tile([P, 4 * P], U8, align_bytes=64)
-        for k in range(N_TILES):
-            cols = slice(k * COLS, (k + 1) * COLS)
+
+        def turn_old_state(rows):
             old_t = []
             for h in range(2):
-                rows = stage.tile([P, COLS], BF16, tag="rows%d" % h)
-                nc.sync.dma_start(out=rows[:], in_=state_in[h][:, cols])
-                words = rows[:].bitcast(F32).rearrange("t (f q) -> t q f", q=4)
+                words = rows[h][:].bitcast(F32).rearrange("t (f q) -> t q f", q=4)
                 bank = psum_in.tile([P, 4, P], F32, tag="in")
                 for q in range(4):
                     nc.tensor.transpose(bank[:, q, :], words[:, q, :], ident_f32[:])
                 old_t.append(bank[:].bitcast(BF16).rearrange("p q (t e) -> p q e t", e=2))
-            old_real_t, old_imag_t = old_t
+            return old_t
 
+        def scale_real(k, old_t):
             new_real_t = work.tile([P, S, P], F32, tag="new_real_t")
             new_imag_t = work.tile([P, S, P], F32, tag="new_imag_t")
             for s in range(S):
                 one = slice(k * S + s, k * S + s + 1)
-                nc.scalar.activation(out=new_real_t[:, s, :], in_=old_real_t[:, s // 2, s % 2, :],
+                nc.scalar.activation(out=new_real_t[:, s, :], in_=old_t[0][:, s // 2, s % 2, :],
                                      func=ACT.Copy, scale=cos_t[:, one])
-                nc.scalar.activation(out=new_imag_t[:, s, :], in_=old_real_t[:, s // 2, s % 2, :],
+                nc.scalar.activation(out=new_imag_t[:, s, :], in_=old_t[0][:, s // 2, s % 2, :],
                                      func=ACT.Copy, scale=sin_t[:, one])
-            for s in range(S):
-                one = slice(k * S + s, k * S + s + 1)
-                nc.vector.scalar_tensor_tensor(
-                    out=new_real_t[:, s, :], in0=old_imag_t[:, s // 2, s % 2, :],
-                    scalar=neg_sin_t[:, one], in1=new_real_t[:, s, :], op0=ALU.mult, op1=ALU.add)
-                nc.vector.scalar_tensor_tensor(
-                    out=new_imag_t[:, s, :], in0=old_imag_t[:, s // 2, s % 2, :],
-                    scalar=cos_t[:, one], in1=new_imag_t[:, s, :], op0=ALU.mult, op1=ALU.add)
-            for s in range(S):
-                one = slice(k * S + s, k * S + s + 1)
-                nc.vector.scalar_tensor_tensor(
-                    out=new_real_t[:, s, :], in0=xin_t[:, k, :], scalar=b_real_t[:, one],
-                    in1=new_real_t[:, s, :], op0=ALU.mult, op1=ALU.add)
-                nc.vector.scalar_tensor_tensor(
-                    out=new_imag_t[:, s, :], in0=xin_t[:, k, :], scalar=b_imag_t[:, one],
-                    in1=new_imag_t[:, s, :], op0=ALU.mult, op1=ALU.add)
+            return new_real_t, new_imag_t
 
-            for h, new_t in enumerate((new_real_t, new_imag_t)):
+        def drive(k):
+            drive_t = [work.tile([P, S, P], F32, tag="drive_real_t", name="drive_real_t"),
+                       work.tile([P, S, P], F32, tag="drive_imag_t", name="drive_imag_t")]
+            y_real_part = small.tile([P, P], F32, tag="y_real_part", bufs=6)
+            nc.gpsimd.tensor_scalar(out=y_real_part[:], in0=xin_t[:, k, :],
+                                    scalar1=drive_y_t[:, k : k + 1], scalar2=0.0,
+                                    op0=ALU.mult, op1=ALU.add)
+            for s in range(S):
+                one = slice(k * S + s, k * S + s + 1)
+                for h in range(2):
+                    nc.gpsimd.tensor_scalar(out=drive_t[h][:, s, :], in0=xin_t[:, k, :],
+                                            scalar1=b_t[h][:, one], scalar2=0.0,
+                                            op0=ALU.mult, op1=ALU.add)
+            return drive_t, y_real_part
+
+        def rotate(k, old_t, new_t, y_real_part):
+            y_imag_part = small.tile([P, P], F32, tag="y_imag_part", bufs=6)
+            for s in range(S):
+                one = slice(k * S + s, k * S + s + 1)
+                old_imag = old_t[1][:, s // 2, s % 2, :]
+                nc.vector.scalar_tensor_tensor(
+                    out=new_t[0][:, s, :], in0=old_imag, scalar=neg_sin_t[:, one],
+                    in1=new_t[0][:, s, :], op0=ALU.mult, op1=ALU.add)
+                if s == 0:
+                    nc.vector.tensor_scalar(out=y_imag_part[:], in0=old_imag,
+                                            scalar1=y_from_imag_t[:, one], scalar2=None,
+                                            op0=ALU.mult)
+                else:
+                    nc.vector.scalar_tensor_tensor(
+                        out=y_imag_part[:], in0=old_imag, scalar=y_from_imag_t[:, one],
+                        in1=y_imag_part[:], op0=ALU.mult, op1=ALU.add)
+                nc.vector.scalar_tensor_tensor(
+                    out=new_t[1][:, s, :], in0=old_imag, scalar=cos_t[:, one],
+                    in1=new_t[1][:, s, :], op0=ALU.mult, op1=ALU.add)
+                nc.vector.scalar_tensor_tensor(
+                    out=y_real_part[:], in0=old_t[0][:, s // 2, s % 2, :],
+                    scalar=y_from_real_t[:, one], in1=y_real_part[:], op0=ALU.mult, op1=ALU.add)
+            return y_imag_part
+
+        def turn_back_and_store(k, new_t, drive_t):
+            for h in range(2):
                 new_rows = leave.tile([P, P, S], F32, tag="new_rows%d" % h)
                 for half_s in range(2):
                     back = psum_out.tile([P, 4, P], F32, tag="out")
                     for j in range(4):
-                        nc.tensor.transpose(back[:, j, :], new_t[:, half_s * 4 + j, :], ident_f32[:])
+                        s = half_s * 4 + j
+                        nc.tensor.matmul(back[:, j, :], lhsT=new_t[h][:, s, :], rhs=ident_f32[:],
+                                         is_transpose=True, start=True, stop=False)
+                        nc.tensor.matmul(back[:, j, :], lhsT=drive_t[h][:, s, :], rhs=ident_f32[:],
+                                         is_transpose=True, start=False, stop=True)
                     nc.scalar.copy(out=new_rows[:, :, half_s * 4 : (half_s + 1) * 4],
                                    in_=back[:].rearrange("t j f -> t f j"))
-                nc.sync.dma_start(out=state_out[h][:, cols],
+                nc.sync.dma_start(out=state_out[h][:, k * COLS : (k + 1) * COLS],
                                   in_=new_rows[:].rearrange("t f s -> t (f s)"))
 
-            y_imag_part = small.tile([P, P], F32, tag="y_imag_part")
-            for s in range(S):
-                one = slice(k * S + s, k * S + s + 1)
-                if s == 0:
-                    nc.vector.tensor_scalar(out=y_t[:, k, :], in0=new_real_t[:, s, :],
-                                            scalar1=c_real_t[:, one], scalar2=None, op0=ALU.mult)
-                    nc.vector.tensor_scalar(out=y_imag_part[:], in0=new_imag_t[:, s, :],
-                                            scalar1=neg_c_imag_t[:, one], scalar2=None, op0=ALU.mult)
-                else:
-                    nc.vector.scalar_tensor_tensor(
-                        out=y_t[:, k, :], in0=new_real_t[:, s, :], scalar=c_real_t[:, one],
-                        in1=y_t[:, k, :], op0=ALU.mult, op1=ALU.add)
-                    nc.vector.scalar_tensor_tensor(
-                        out=y_imag_part[:], in0=new_imag_t[:, s, :], scalar=neg_c_imag_t[:, one],
-                        in1=y_imag_part[:], op0=ALU.mult, op1=ALU.add)
-            nc.vector.tensor_tensor(out=y_t[:, k, :], in0=y_t[:, k, :], in1=y_imag_part[:], op=ALU.add)
+        def quantise_y(c, y_parts):
+            y_back = psum_out.tile([P, 4, P], F32, tag="out")
+            for q in range(4):
+                real_part, imag_part = y_parts[q]
+                nc.tensor.matmul(y_back[:, q, :], lhsT=real_part[:], rhs=ident_f32[:],
+                                 is_transpose=True, start=True, stop=False)
+                nc.tensor.matmul(y_back[:, q, :], lhsT=imag_part[:], rhs=ident_f32[:],
+                                 is_transpose=True, start=False, stop=True)
+            y_rows = small.tile([P, 512], BF16, tag="y_rows")
+            nc.scalar.copy(out=y_rows[:], in_=y_back[:].rearrange("t q f -> t (q f)"))
+            y_words = y_rows[:].bitcast(F32)
+            y_bank = psum_out.tile([P, 2, P], F32, tag="out")
+            for u in range(2):
+                nc.tensor.transpose(y_bank[:, u, :], y_words[:, u : 256 : 2], ident_f32[:])
+            nc.scalar.copy(out=y_grouped[:, c, :, :].bitcast(F32),
+                           in_=y_bank[:].rearrange("p u t -> p t u"))
+            nc.vector.quantize_mx(out=y_codes[:, c * P : (c + 1) * P].bitcast(FP8X4),
+                                  scales=y_scales[:, c * P : (c + 1) * P],
+                                  in_=y_grouped[:, c, :, :].rearrange("p t q -> p (t q)"))
 
+        w_in_rows = {0: load_w_in(0), 1: load_w_in(1)}
+        rows = {0: load_state(0)}
+        b_raw = [load_coefficients(nc, tables, B_real, "b_real_raw"),
+                 load_coefficients(nc, tables, B_imag, "b_imag_raw")]
+        c_raw = [load_coefficients(nc, tables, C_real, "c_real_raw"),
+                 load_coefficients(nc, tables, C_imag, "c_imag_raw")]
+        rows[1] = load_state(1)
+        w_in_rows[2] = load_w_in(2)
+
+        make_x_in(0, w_in_rows[0])
+        old = {0: turn_old_state(rows[0])}
+        scaled = {0: scale_real(0, old[0])}
+
+        b_t = [tables.tile([P, n_coef], F32, name="b_real_t"),
+               tables.tile([P, n_coef], F32, name="b_imag_t")]
+        for h in range(2):
+            nc.vector.tensor_copy(out=b_t[h][:], in_=b_raw[h][:])
+
+        def combine(name, first, first_sign, second, second_sign, with_first, with_second):
+            part = tables.tile([P, n_coef], F32, tag="part", bufs=2)
+            total = tables.tile([P, n_coef], F32, name=name)
+            nc.vector.scalar_tensor_tensor(out=part[:], in0=first[:], scalar=first_sign,
+                                           in1=with_first[:], op0=ALU.mult, op1=ALU.mult)
+            nc.vector.scalar_tensor_tensor(out=total[:], in0=second[:], scalar=second_sign,
+                                           in1=with_second[:], op0=ALU.mult, op1=ALU.mult)
+            nc.vector.tensor_tensor(out=total[:], in0=total[:], in1=part[:], op=ALU.add)
+            return total
+
+        y_from_imag_t = combine("y_from_imag_t", c_raw[0], -1.0, c_raw[1], -1.0, sin_t, cos_t)
+        y_from_real_t = combine("y_from_real_t", c_raw[0], 1.0, c_raw[1], -1.0, cos_t, sin_t)
+        y_from_drive = combine("y_from_drive", c_raw[0], 1.0, c_raw[1], -1.0, b_t[0], b_t[1])
+        drive_y_t = tables.tile([P, N_TILES], F32)
+        nc.vector.tensor_reduce(out=drive_y_t[:],
+                                in_=y_from_drive[:].rearrange("p (k s) -> p k s", s=S),
+                                axis=AX.X, op=ALU.add)
+        norm_w_all = consts.tile([P, D], BF16)
+
+        driven = {0: drive(0)}
+        make_x_in(1, w_in_rows[1])
+        w_out_rows = {}
+        y_parts = {}
+        for k in range(N_TILES):
+            if k + 2 < N_TILES:
+                rows[k + 2] = load_state(k + 2)
+            if k + 3 < N_TILES:
+                w_in_rows[k + 3] = load_w_in(k + 3)
+            if k % 2 == 0:
+                w_out_rows[k // 2] = load_w_out(k // 2)
+            if k == 3:
+                nc.sync.dma_start(out=norm_w_all[:], in_=norm_w.partition_broadcast(P))
+            if k + 1 < N_TILES:
+                old[k + 1] = turn_old_state(rows[k + 1])
+                scaled[k + 1] = scale_real(k + 1, old[k + 1])
+                driven[k + 1] = drive(k + 1)
+            if k + 2 < N_TILES:
+                make_x_in(k + 2, w_in_rows[k + 2])
+            y_imag_part = rotate(k, old[k], scaled[k], driven[k][1])
+            y_parts[k % 4] = (driven[k][1], y_imag_part)
+            prepare_w_out(k // 2, k % 2, w_out_rows[k // 2])
+            turn_back_and_store(k, scaled[k], driven[k][0])
             if k % 4 == 3:
-                c = k // 4
-                y_back = psum_out.tile([P, 4, P], F32, tag="out")
-                for q in range(4):
-                    nc.tensor.transpose(y_back[:, q, :], y_t[:, c * 4 + q, :], ident_f32[:])
-                y_rows = small.tile([P, 512], BF16, tag="y_rows")
-                nc.scalar.copy(out=y_rows[:], in_=y_back[:].rearrange("t q f -> t (q f)"))
-                y_words = y_rows[:].bitcast(F32)
-                y_bank = psum_out.tile([P, 2, P], F32, tag="out")
-                for u in range(2):
-                    nc.tensor.transpose(y_bank[:, u, :], y_words[:, u : 256 : 2], ident_f32[:])
-                nc.scalar.copy(out=y_grouped[:, c, :, :].bitcast(F32),
-                               in_=y_bank[:].rearrange("p u t -> p t u"))
-                nc.vector.quantize_mx(out=y_codes[:, c * P : (c + 1) * P].bitcast(FP8X4),
-                                      scales=y_scales[:, c * P : (c + 1) * P],
-                                      in_=y_grouped[:, c, :, :].rearrange("p t q -> p (t q)"))
-            if k % 4 == 1:
-                prepare_w_out(k // 4)
+                quantise_y(k // 4, y_parts)
 
         o_banks = []
         for nb in range(2):
-            o_bank = psum_in.tile([P, 2, 256], F32, tag="in")
+            o_bank = psum_in.tile([P, 4, P], F32, tag="in")
             o_banks.append(o_bank)
-            for i in range(2):
-                piece = nb * 2 + i
+            for i in range(4):
                 for c in range(4):
-                    cols = slice(piece * PIECE_WORDS + c * 256, piece * PIECE_WORDS + (c + 1) * 256)
+                    cols = slice(c * P, (c + 1) * P)
                     nc.tensor.matmul_mx(out=o_bank[:, i, :],
-                                        lhsT=y_codes[:, c * P : (c + 1) * P].bitcast(FP8X4),
-                                        lhsT_scale=y_scales[:, c * P : (c + 1) * P],
-                                        rhs=wo_codes[:, cols].bitcast(FP8X4),
-                                        rhs_scale=wo_scales[:, cols],
+                                        lhsT=y_codes[:, cols].bitcast(FP8X4),
+                                        lhsT_scale=y_scales[:, cols],
+                                        rhs=wo_codes[:, nb * 4 + i, cols].bitcast(FP8X4),
+                                        rhs_scale=wo_scales[:, nb * 4 + i, cols],
                                         start=(c == 0), stop=(c == 3))
 
         sums = small.tile([P, 2], F32)

@@ -30,20 +30,16 @@ TWO_PI_LO = 2.0 * math.pi - TWO_PI_HI - TWO_PI_MID
 PI_BELOW = 3.1415925
 
 
-def load_coefficients(nc, pool, coeff, name):
-    raw = pool.tile([P, N_TILES * S], BF16, name=name)
-    nc.sync.dma_start(
-        out=raw[:].rearrange("p (k s) -> p k s", s=S),
-        in_=coeff.rearrange("c d s -> (c d) s").rearrange("(k p) s -> p k s", p=P))
-    return raw
-
-
-def transpose_word_blocks(nc, psum, ident_f32, rows_bf16):
-    words = rows_bf16.bitcast(F32)
+def transpose_word_blocks(nc, pool, psum, ident_f32, rows_bf16):
+    sorted_words = pool.tile([P, 2, 2, P], F32, tag="sorted_words")
+    for a in range(2):
+        nc.vector.tensor_copy(
+            out=sorted_words[:, a, :, :].rearrange("r u (g i) -> r g u i", i=4),
+            in_=rows_bf16.bitcast(F32)[:, a * 256 : (a + 1) * 256].rearrange(
+                "r (g i u) -> r g u i", i=4, u=2))
     bank = psum.tile([P, 4, P], F32, tag="out")
     for b in range(4):
-        nc.tensor.transpose(bank[:, b, :], words[:, 256 * (b // 2) + b % 2 : 256 * (b // 2 + 1) : 2],
-                            ident_f32[:])
+        nc.tensor.transpose(bank[:, b, :], sorted_words[:, b // 2, b % 2, :], ident_f32[:])
     return bank
 
 
@@ -68,13 +64,19 @@ def tile_recursivemamba130m_kernel(
 
         ident_f32 = consts.tile([P, P], F32)
         make_identity(nc, ident_f32[:])
+        ident_bf16 = consts.tile([P, P], BF16)
+        make_identity(nc, ident_bf16[:])
 
         state_in = [real_state.rearrange("b l c d s -> (b l) (c d s)"),
                     imag_state.rearrange("b l c d s -> (b l) (c d s)")]
         state_out = [out_1.rearrange("b l c d s -> (b l) (c d s)"),
                      out_2.rearrange("b l c d s -> (b l) (c d s)")]
 
-        theta = load_coefficients(nc, tables, A_theta, "theta")
+        coef_rows = tables.tile([P, COLS], BF16)
+        nc.vector.memset(coef_rows[64:P, :], 0.0)
+        for i, coeff in enumerate((A_theta, B_real, B_imag, C_real, C_imag)):
+            nc.sync.dma_start(out=coef_rows[i * N_TILES : (i + 1) * N_TILES, :],
+                              in_=coeff.rearrange("c (k p) s -> (c k) (p s)", p=P))
         x_sb = consts.tile([P, D], BF16)
         nc.sync.dma_start(out=x_sb[:], in_=x.rearrange("b l d -> (b l) d"))
 
@@ -97,14 +99,23 @@ def tile_recursivemamba130m_kernel(
             return rows
 
         n_coef = N_TILES * S
+        coef_bank = psum_in.tile([P, S, P], BF16, tag="in")
+        for s in range(S):
+            nc.tensor.transpose(coef_bank[:, s, :], coef_rows[:, s : COLS : S], ident_bf16[:])
+        coefs = tables.tile([P, 5, n_coef], F32)
+        nc.scalar.copy(out=coefs[:].rearrange("p i (k s) -> p (i k) s", s=S),
+                       in_=coef_bank[:, :, 0 : 5 * N_TILES].rearrange("p s j -> p j s"))
+        theta = coefs[:, 0, :]
+        b_t = [coefs[:, 1, :], coefs[:, 2, :]]
+        c_t = [coefs[:, 3, :], coefs[:, 4, :]]
         turns = tables.tile([P, n_coef], F32)
-        nc.vector.tensor_scalar(out=turns[:], in0=theta[:], scalar1=1.0 / (2.0 * math.pi),
+        nc.vector.tensor_scalar(out=turns[:], in0=theta, scalar1=1.0 / (2.0 * math.pi),
                                 scalar2=ROUND_MAGIC, op0=ALU.mult, op1=ALU.add)
         nc.vector.tensor_scalar(out=turns[:], in0=turns[:], scalar1=ROUND_MAGIC, scalar2=None,
                                 op0=ALU.subtract)
         reduced = tables.tile([P, n_coef], F32)
         nc.vector.scalar_tensor_tensor(out=reduced[:], in0=turns[:], scalar=-TWO_PI_HI,
-                                       in1=theta[:], op0=ALU.mult, op1=ALU.add)
+                                       in1=theta, op0=ALU.mult, op1=ALU.add)
         nc.vector.scalar_tensor_tensor(out=reduced[:], in0=turns[:], scalar=-TWO_PI_MID,
                                        in1=reduced[:], op0=ALU.mult, op1=ALU.add)
         nc.vector.scalar_tensor_tensor(out=reduced[:], in0=turns[:], scalar=-TWO_PI_LO,
@@ -123,7 +134,7 @@ def tile_recursivemamba130m_kernel(
         nc.vector.tensor_scalar(out=neg_sin_t[:], in0=sin_t[:], scalar1=-1.0, scalar2=None,
                                 op0=ALU.mult)
 
-        x_bank = transpose_word_blocks(nc, psum_out, ident_f32, x_sb[:])
+        x_bank = transpose_word_blocks(nc, work, psum_out, ident_f32, x_sb[:])
         x_grouped = mxops.tile([P, 2, P, 4], BF16, align_bytes=64)
         nc.scalar.copy(out=x_grouped[:].bitcast(F32),
                        in_=x_bank[:].rearrange("p (a u) n -> p a n u", u=2))
@@ -135,7 +146,7 @@ def tile_recursivemamba130m_kernel(
         xin_t = mid.tile([P, N_TILES, P], F32)
 
         def make_x_in(k, w_rows):
-            w_bank = transpose_word_blocks(nc, psum_out, ident_f32, w_rows[:])
+            w_bank = transpose_word_blocks(nc, work, psum_out, ident_f32, w_rows[:])
             w_grouped = wgroup.tile([P, 2, P, 4], BF16, tag="w_in_grouped", align_bytes=64)
             nc.scalar.copy(out=w_grouped[:].bitcast(F32),
                            in_=w_bank[:].rearrange("p (a u) n -> p a n u", u=2))
@@ -156,11 +167,11 @@ def tile_recursivemamba130m_kernel(
         wo_scales = mxops.tile([P, 8, 4 * P], U8, align_bytes=64)
 
         def prepare_w_out(r, half_k, wo_rows):
-            wo_bank = transpose_word_blocks(nc, psum_out, ident_f32,
+            wo_bank = transpose_word_blocks(nc, work, psum_out, ident_f32,
                                             wo_rows[:, half_k * D : (half_k + 1) * D])
             wo_grouped = wgroup.tile([P, 2, P, 4], BF16, tag="w_out_grouped", align_bytes=64)
-            nc.vector.tensor_copy(out=wo_grouped[:].bitcast(F32),
-                                  in_=wo_bank[:].rearrange("p (a u) n -> p a n u", u=2))
+            nc.scalar.copy(out=wo_grouped[:].bitcast(F32),
+                           in_=wo_bank[:].rearrange("p (a u) n -> p a n u", u=2))
             words = slice(half_k * 2 * P, (half_k + 1) * 2 * P)
             nc.vector.quantize_mx(out=wo_codes[:, r, words].bitcast(FP8X4),
                                   scales=wo_scales[:, r, words],
@@ -173,7 +184,10 @@ def tile_recursivemamba130m_kernel(
         def turn_old_state(rows):
             old_t = []
             for h in range(2):
-                words = rows[h][:].bitcast(F32).rearrange("t (f q) -> t q f", q=4)
+                words = work.tile([P, 4, P], F32, tag="sorted_state")
+                nc.vector.tensor_copy(
+                    out=words[:].rearrange("t q (g i) -> t g q i", i=4),
+                    in_=rows[h][:].bitcast(F32).rearrange("t (g i q) -> t g q i", i=4, q=4))
                 bank = psum_in.tile([P, 4, P], F32, tag="in")
                 for q in range(4):
                     nc.tensor.transpose(bank[:, q, :], words[:, q, :], ident_f32[:])
@@ -195,9 +209,8 @@ def tile_recursivemamba130m_kernel(
             drive_t = [work.tile([P, S, P], F32, tag="drive_real_t", name="drive_real_t"),
                        work.tile([P, S, P], F32, tag="drive_imag_t", name="drive_imag_t")]
             y_real_part = small.tile([P, P], F32, tag="y_real_part", bufs=6)
-            nc.gpsimd.tensor_scalar(out=y_real_part[:], in0=xin_t[:, k, :],
-                                    scalar1=drive_y_t[:, k : k + 1], scalar2=0.0,
-                                    op0=ALU.mult, op1=ALU.add)
+            nc.vector.tensor_scalar(out=y_real_part[:], in0=xin_t[:, k, :],
+                                    scalar1=drive_y_t[:, k : k + 1], scalar2=None, op0=ALU.mult)
             for s in range(S):
                 one = slice(k * S + s, k * S + s + 1)
                 for h in range(2):
@@ -268,10 +281,6 @@ def tile_recursivemamba130m_kernel(
 
         w_in_rows = {0: load_w_in(0), 1: load_w_in(1)}
         rows = {0: load_state(0)}
-        b_raw = [load_coefficients(nc, tables, B_real, "b_real_raw"),
-                 load_coefficients(nc, tables, B_imag, "b_imag_raw")]
-        c_raw = [load_coefficients(nc, tables, C_real, "c_real_raw"),
-                 load_coefficients(nc, tables, C_imag, "c_imag_raw")]
         rows[1] = load_state(1)
         w_in_rows[2] = load_w_in(2)
 
@@ -279,24 +288,19 @@ def tile_recursivemamba130m_kernel(
         old = {0: turn_old_state(rows[0])}
         scaled = {0: scale_real(0, old[0])}
 
-        b_t = [tables.tile([P, n_coef], F32, name="b_real_t"),
-               tables.tile([P, n_coef], F32, name="b_imag_t")]
-        for h in range(2):
-            nc.vector.tensor_copy(out=b_t[h][:], in_=b_raw[h][:])
-
         def combine(name, first, first_sign, second, second_sign, with_first, with_second):
             part = tables.tile([P, n_coef], F32, tag="part", bufs=2)
             total = tables.tile([P, n_coef], F32, name=name)
-            nc.vector.scalar_tensor_tensor(out=part[:], in0=first[:], scalar=first_sign,
-                                           in1=with_first[:], op0=ALU.mult, op1=ALU.mult)
-            nc.vector.scalar_tensor_tensor(out=total[:], in0=second[:], scalar=second_sign,
-                                           in1=with_second[:], op0=ALU.mult, op1=ALU.mult)
+            nc.vector.scalar_tensor_tensor(out=part[:], in0=first, scalar=first_sign,
+                                           in1=with_first, op0=ALU.mult, op1=ALU.mult)
+            nc.vector.scalar_tensor_tensor(out=total[:], in0=second, scalar=second_sign,
+                                           in1=with_second, op0=ALU.mult, op1=ALU.mult)
             nc.vector.tensor_tensor(out=total[:], in0=total[:], in1=part[:], op=ALU.add)
             return total
 
-        y_from_imag_t = combine("y_from_imag_t", c_raw[0], -1.0, c_raw[1], -1.0, sin_t, cos_t)
-        y_from_real_t = combine("y_from_real_t", c_raw[0], 1.0, c_raw[1], -1.0, cos_t, sin_t)
-        y_from_drive = combine("y_from_drive", c_raw[0], 1.0, c_raw[1], -1.0, b_t[0], b_t[1])
+        y_from_imag_t = combine("y_from_imag_t", c_t[0], -1.0, c_t[1], -1.0, sin_t[:], cos_t[:])
+        y_from_real_t = combine("y_from_real_t", c_t[0], 1.0, c_t[1], -1.0, cos_t[:], sin_t[:])
+        y_from_drive = combine("y_from_drive", c_t[0], 1.0, c_t[1], -1.0, b_t[0], b_t[1])
         drive_y_t = tables.tile([P, N_TILES], F32)
         nc.vector.tensor_reduce(out=drive_y_t[:],
                                 in_=y_from_drive[:].rearrange("p (k s) -> p k s", s=S),

@@ -30,16 +30,12 @@ TWO_PI_LO = 2.0 * math.pi - TWO_PI_HI - TWO_PI_MID
 PI_BELOW = 3.1415925
 
 
-def transpose_word_blocks(nc, pool, psum, ident_f32, rows_bf16):
-    sorted_words = pool.tile([P, 2, 2, P], F32, tag="sorted_words")
-    for a in range(2):
-        nc.vector.tensor_copy(
-            out=sorted_words[:, a, :, :].rearrange("r u (g i) -> r g u i", i=4),
-            in_=rows_bf16.bitcast(F32)[:, a * 256 : (a + 1) * 256].rearrange(
-                "r (g i u) -> r g u i", i=4, u=2))
+def transpose_word_blocks(nc, psum, ident_f32, rows_bf16):
+    words = rows_bf16.bitcast(F32)
     bank = psum.tile([P, 4, P], F32, tag="out")
     for b in range(4):
-        nc.tensor.transpose(bank[:, b, :], sorted_words[:, b // 2, b % 2, :], ident_f32[:])
+        nc.tensor.transpose(bank[:, b, :], words[:, 256 * (b // 2) + b % 2 : 256 * (b // 2 + 1) : 2],
+                            ident_f32[:])
     return bank
 
 
@@ -51,7 +47,7 @@ def tile_recursivemamba130m_kernel(
     with ExitStack() as ctx:
         consts = ctx.enter_context(tc.tile_pool(name="consts", bufs=1))
         tables = ctx.enter_context(tc.tile_pool(name="tables", bufs=1))
-        wstage = ctx.enter_context(tc.tile_pool(name="wstage", bufs=4))
+        wstage = ctx.enter_context(tc.tile_pool(name="wstage", bufs=5))
         wgroup = ctx.enter_context(tc.tile_pool(name="wgroup", bufs=3))
         mxops = ctx.enter_context(tc.tile_pool(name="mxops", bufs=1))
         mid = ctx.enter_context(tc.tile_pool(name="mid", bufs=1))
@@ -134,7 +130,7 @@ def tile_recursivemamba130m_kernel(
         nc.vector.tensor_scalar(out=neg_sin_t[:], in0=sin_t[:], scalar1=-1.0, scalar2=None,
                                 op0=ALU.mult)
 
-        x_bank = transpose_word_blocks(nc, work, psum_out, ident_f32, x_sb[:])
+        x_bank = transpose_word_blocks(nc, psum_out, ident_f32, x_sb[:])
         x_grouped = mxops.tile([P, 2, P, 4], BF16, align_bytes=64)
         nc.scalar.copy(out=x_grouped[:].bitcast(F32),
                        in_=x_bank[:].rearrange("p (a u) n -> p a n u", u=2))
@@ -145,15 +141,20 @@ def tile_recursivemamba130m_kernel(
 
         xin_t = mid.tile([P, N_TILES, P], F32)
 
-        def make_x_in(k, w_rows):
-            w_bank = transpose_word_blocks(nc, work, psum_out, ident_f32, w_rows[:])
-            w_grouped = wgroup.tile([P, 2, P, 4], BF16, tag="w_in_grouped", align_bytes=64)
-            nc.scalar.copy(out=w_grouped[:].bitcast(F32),
-                           in_=w_bank[:].rearrange("p (a u) n -> p a n u", u=2))
+        def group_words(bank, tag):
+            grouped = wgroup.tile([P, 2, P, 4], BF16, tag=tag, align_bytes=64)
+            nc.scalar.copy(out=grouped[:].bitcast(F32),
+                           in_=bank[:].rearrange("p (a u) n -> p a n u", u=2))
+            return grouped
+
+        def quantise_w_in(w_grouped):
             codes = wgroup.tile([P, 2 * P], U32, tag="w_in_codes", align_bytes=64)
             scales = wgroup.tile([P, 2 * P], U8, tag="w_in_scales", align_bytes=64)
             nc.vector.quantize_mx(out=codes[:].bitcast(FP8X4), scales=scales[:],
                                   in_=w_grouped[:].rearrange("p a n j -> p (a n j)"))
+            return codes, scales
+
+        def multiply_x(codes, scales):
             xin_bank = psum_out.tile([P, P], F32, tag="out")
             for a in range(2):
                 cols = slice(a * P, (a + 1) * P)
@@ -161,17 +162,12 @@ def tile_recursivemamba130m_kernel(
                                     lhsT_scale=scales[:, cols],
                                     rhs=x_codes[:, cols].bitcast(FP8X4), rhs_scale=x_scales[:, cols],
                                     start=(a == 0), stop=(a == 1))
-            nc.scalar.copy(out=xin_t[:, k, :], in_=xin_bank[:])
+            return xin_bank
 
         wo_codes = mxops.tile([P, 8, 4 * P], U32, align_bytes=64)
         wo_scales = mxops.tile([P, 8, 4 * P], U8, align_bytes=64)
 
-        def prepare_w_out(r, half_k, wo_rows):
-            wo_bank = transpose_word_blocks(nc, work, psum_out, ident_f32,
-                                            wo_rows[:, half_k * D : (half_k + 1) * D])
-            wo_grouped = wgroup.tile([P, 2, P, 4], BF16, tag="w_out_grouped", align_bytes=64)
-            nc.scalar.copy(out=wo_grouped[:].bitcast(F32),
-                           in_=wo_bank[:].rearrange("p (a u) n -> p a n u", u=2))
+        def quantise_w_out(r, half_k, wo_grouped):
             words = slice(half_k * 2 * P, (half_k + 1) * 2 * P)
             nc.vector.quantize_mx(out=wo_codes[:, r, words].bitcast(FP8X4),
                                   scales=wo_scales[:, r, words],
@@ -184,10 +180,7 @@ def tile_recursivemamba130m_kernel(
         def turn_old_state(rows):
             old_t = []
             for h in range(2):
-                words = work.tile([P, 4, P], F32, tag="sorted_state")
-                nc.vector.tensor_copy(
-                    out=words[:].rearrange("t q (g i) -> t g q i", i=4),
-                    in_=rows[h][:].bitcast(F32).rearrange("t (g i q) -> t g q i", i=4, q=4))
+                words = rows[h][:].bitcast(F32).rearrange("t (f q) -> t q f", q=4)
                 bank = psum_in.tile([P, 4, P], F32, tag="in")
                 for q in range(4):
                     nc.tensor.transpose(bank[:, q, :], words[:, q, :], ident_f32[:])
@@ -208,19 +201,19 @@ def tile_recursivemamba130m_kernel(
         def drive(k):
             drive_t = [work.tile([P, S, P], F32, tag="drive_real_t", name="drive_real_t"),
                        work.tile([P, S, P], F32, tag="drive_imag_t", name="drive_imag_t")]
-            y_real_part = small.tile([P, P], F32, tag="y_real_part", bufs=6)
-            nc.vector.tensor_scalar(out=y_real_part[:], in0=xin_t[:, k, :],
-                                    scalar1=drive_y_t[:, k : k + 1], scalar2=None, op0=ALU.mult)
             for s in range(S):
                 one = slice(k * S + s, k * S + s + 1)
                 for h in range(2):
                     nc.gpsimd.tensor_scalar(out=drive_t[h][:, s, :], in0=xin_t[:, k, :],
                                             scalar1=b_t[h][:, one], scalar2=0.0,
                                             op0=ALU.mult, op1=ALU.add)
-            return drive_t, y_real_part
+            return drive_t
 
-        def rotate(k, old_t, new_t, y_real_part):
+        def rotate(k, old_t, new_t):
+            y_real_part = small.tile([P, P], F32, tag="y_real_part", bufs=6)
             y_imag_part = small.tile([P, P], F32, tag="y_imag_part", bufs=6)
+            nc.vector.tensor_scalar(out=y_real_part[:], in0=xin_t[:, k, :],
+                                    scalar1=drive_y_t[:, k : k + 1], scalar2=None, op0=ALU.mult)
             for s in range(S):
                 one = slice(k * S + s, k * S + s + 1)
                 old_imag = old_t[1][:, s // 2, s % 2, :]
@@ -241,7 +234,7 @@ def tile_recursivemamba130m_kernel(
                 nc.vector.scalar_tensor_tensor(
                     out=y_real_part[:], in0=old_t[0][:, s // 2, s % 2, :],
                     scalar=y_from_real_t[:, one], in1=y_real_part[:], op0=ALU.mult, op1=ALU.add)
-            return y_imag_part
+            return y_real_part, y_imag_part
 
         def turn_back_and_store(k, new_t, drive_t):
             for h in range(2):
@@ -259,7 +252,7 @@ def tile_recursivemamba130m_kernel(
                 nc.sync.dma_start(out=state_out[h][:, k * COLS : (k + 1) * COLS],
                                   in_=new_rows[:].rearrange("t f s -> t (f s)"))
 
-        def quantise_y(c, y_parts):
+        def round_y(y_parts):
             y_back = psum_out.tile([P, 4, P], F32, tag="out")
             for q in range(4):
                 real_part, imag_part = y_parts[q]
@@ -269,24 +262,20 @@ def tile_recursivemamba130m_kernel(
                                  is_transpose=True, start=False, stop=True)
             y_rows = small.tile([P, 512], BF16, tag="y_rows")
             nc.scalar.copy(out=y_rows[:], in_=y_back[:].rearrange("t q f -> t (q f)"))
+            return y_rows
+
+        def group_y(c, y_rows):
             y_words = y_rows[:].bitcast(F32)
             y_bank = psum_out.tile([P, 2, P], F32, tag="out")
             for u in range(2):
                 nc.tensor.transpose(y_bank[:, u, :], y_words[:, u : 256 : 2], ident_f32[:])
             nc.scalar.copy(out=y_grouped[:, c, :, :].bitcast(F32),
                            in_=y_bank[:].rearrange("p u t -> p t u"))
+
+        def quantise_y(c):
             nc.vector.quantize_mx(out=y_codes[:, c * P : (c + 1) * P].bitcast(FP8X4),
                                   scales=y_scales[:, c * P : (c + 1) * P],
                                   in_=y_grouped[:, c, :, :].rearrange("p t q -> p (t q)"))
-
-        w_in_rows = {0: load_w_in(0), 1: load_w_in(1)}
-        rows = {0: load_state(0)}
-        rows[1] = load_state(1)
-        w_in_rows[2] = load_w_in(2)
-
-        make_x_in(0, w_in_rows[0])
-        old = {0: turn_old_state(rows[0])}
-        scaled = {0: scale_real(0, old[0])}
 
         def combine(name, first, first_sign, second, second_sign, with_first, with_second):
             part = tables.tile([P, n_coef], F32, tag="part", bufs=2)
@@ -307,31 +296,61 @@ def tile_recursivemamba130m_kernel(
                                 axis=AX.X, op=ALU.add)
         norm_w_all = consts.tile([P, D], BF16)
 
-        driven = {0: drive(0)}
-        make_x_in(1, w_in_rows[1])
-        w_out_rows = {}
-        y_parts = {}
-        for k in range(N_TILES):
-            if k + 2 < N_TILES:
-                rows[k + 2] = load_state(k + 2)
-            if k + 3 < N_TILES:
-                w_in_rows[k + 3] = load_w_in(k + 3)
-            if k % 2 == 0:
-                w_out_rows[k // 2] = load_w_out(k // 2)
-            if k == 3:
-                nc.sync.dma_start(out=norm_w_all[:], in_=norm_w.partition_broadcast(P))
-            if k + 1 < N_TILES:
-                old[k + 1] = turn_old_state(rows[k + 1])
-                scaled[k + 1] = scale_real(k + 1, old[k + 1])
-                driven[k + 1] = drive(k + 1)
-            if k + 2 < N_TILES:
-                make_x_in(k + 2, w_in_rows[k + 2])
-            y_imag_part = rotate(k, old[k], scaled[k], driven[k][1])
-            y_parts[k % 4] = (driven[k][1], y_imag_part)
-            prepare_w_out(k // 2, k % 2, w_out_rows[k // 2])
-            turn_back_and_store(k, scaled[k], driven[k][0])
-            if k % 4 == 3:
-                quantise_y(k // 4, y_parts)
+        w_in_rows, w_out_rows, rows = {}, {}, {}
+        for k in range(3):
+            w_in_rows[k] = load_w_in(k)
+            rows[k] = load_state(k)
+        w_out_rows[0] = load_w_out(0)
+
+        w_grouped, wo_grouped, w_quant = {}, {}, {}
+        xin_bank, old, scaled, driven, y_parts, y_rows = {}, {}, {}, {}, {}, {}
+        ordered = (mybir.EngineType.PE, mybir.EngineType.Activation, mybir.EngineType.DVE,
+                   mybir.EngineType.Pool)
+        with tc.manual_schedule(engines=set(ordered)):
+            for i in range(-4, N_TILES + 3):
+                if 3 <= i + 4 < N_TILES:
+                    rows[i + 4] = load_state(i + 4)
+                if 3 <= i + 7 < N_TILES:
+                    w_in_rows[i + 7] = load_w_in(i + 7)
+                if i >= 0 and i % 2 == 0 and i // 2 + 1 < S:
+                    w_out_rows[i // 2 + 1] = load_w_out(i // 2 + 1)
+                if i == 10:
+                    nc.sync.dma_start(out=norm_w_all[:], in_=norm_w.partition_broadcast(P))
+
+                if i + 4 < N_TILES:
+                    w_bank = transpose_word_blocks(nc, psum_out, ident_f32, w_in_rows[i + 4][:])
+                if 0 <= i < N_TILES:
+                    wo_bank = transpose_word_blocks(
+                        nc, psum_out, ident_f32,
+                        w_out_rows[i // 2][:, (i % 2) * D : (i % 2 + 1) * D])
+                if 0 <= i + 2 < N_TILES:
+                    nc.scalar.copy(out=xin_t[:, i + 2, :], in_=xin_bank[i + 2][:])
+                if i + 4 < N_TILES:
+                    w_grouped[i + 4] = group_words(w_bank, "w_in_grouped")
+                if 0 <= i < N_TILES:
+                    wo_grouped[i] = group_words(wo_bank, "w_out_grouped")
+                if 0 <= i + 1 < N_TILES:
+                    old[i + 1] = turn_old_state(rows[i + 1])
+                if 0 <= i + 3 < N_TILES:
+                    w_quant[i + 3] = quantise_w_in(w_grouped[i + 3])
+                if 0 <= i - 1 < N_TILES:
+                    quantise_w_out((i - 1) // 2, (i - 1) % 2, wo_grouped[i - 1])
+                if i >= 6 and i % 4 == 2:
+                    quantise_y(i // 4 - 1)
+                if 0 <= i + 1 < N_TILES:
+                    driven[i + 1] = drive(i + 1)
+                if 0 <= i - 1 < N_TILES:
+                    turn_back_and_store(i - 1, scaled[i - 1], driven[i - 1])
+                if i >= 4 and i % 4 == 0:
+                    y_rows[i // 4 - 1] = round_y(y_parts)
+                if i >= 5 and i % 4 == 1:
+                    group_y(i // 4 - 1, y_rows[i // 4 - 1])
+                if 0 <= i + 3 < N_TILES:
+                    xin_bank[i + 3] = multiply_x(*w_quant[i + 3])
+                if 0 <= i + 1 < N_TILES:
+                    scaled[i + 1] = scale_real(i + 1, old[i + 1])
+                if 0 <= i < N_TILES:
+                    y_parts[i % 4] = rotate(i, old[i], scaled[i])
 
         o_banks = []
         for nb in range(2):

@@ -39,6 +39,15 @@ def transpose_word_blocks(nc, psum, ident_f32, rows_bf16):
     return bank
 
 
+def transpose_w_out_words(nc, psum, ident_f32, pair_rows, c):
+    bank = psum.tile([P, 2, 2, P], F32, tag="out")
+    for r in range(2):
+        words = pair_rows[:, r, c * 512 : (c + 1) * 512].bitcast(F32)
+        for u in range(2):
+            nc.tensor.transpose(bank[:, u, r, :], words[:, u : 256 : 2], ident_f32[:])
+    return bank
+
+
 def tile_recursivemamba130m_kernel(
     tc, x, real_state, imag_state, W_in, A_theta, B_real, B_imag, C_real, C_imag, W_out, norm_w,
     out_0, out_1, out_2,
@@ -52,7 +61,7 @@ def tile_recursivemamba130m_kernel(
         mxops = ctx.enter_context(tc.tile_pool(name="mxops", bufs=1))
         mid = ctx.enter_context(tc.tile_pool(name="mid", bufs=1))
         small = ctx.enter_context(tc.tile_pool(name="small", bufs=2))
-        stage = ctx.enter_context(tc.tile_pool(name="stage", bufs=6))
+        stage = ctx.enter_context(tc.tile_pool(name="stage", bufs=5))
         work = ctx.enter_context(tc.tile_pool(name="work", bufs=3))
         leave = ctx.enter_context(tc.tile_pool(name="leave", bufs=3))
         psum_in = ctx.enter_context(tc.psum_pool(name="psum_in", bufs=4))
@@ -89,56 +98,29 @@ def tile_recursivemamba130m_kernel(
             nc.sync.dma_start(out=rows[:], in_=W_in[k * P : (k + 1) * P, :])
             return rows
 
-        def load_w_out(r):
-            rows = wstage.tile([P, CD], BF16, tag="w_out_rows")
-            nc.sync.dma_start(out=rows[:], in_=W_out[r * P : (r + 1) * P, :])
+        def load_w_out(pair):
+            rows = wstage.tile([P, 2, CD], BF16, tag="w_out_rows", bufs=3)
+            nc.sync.dma_start(
+                out=rows[:],
+                in_=W_out[pair * 2 * P : (pair + 1) * 2 * P, :].rearrange("(r p) k -> p r k", p=P))
             return rows
 
-        n_coef = N_TILES * S
-        coef_bank = psum_in.tile([P, S, P], BF16, tag="in")
-        for s in range(S):
-            nc.tensor.transpose(coef_bank[:, s, :], coef_rows[:, s : COLS : S], ident_bf16[:])
-        coefs = tables.tile([P, 5, n_coef], F32)
-        nc.scalar.copy(out=coefs[:].rearrange("p i (k s) -> p (i k) s", s=S),
-                       in_=coef_bank[:, :, 0 : 5 * N_TILES].rearrange("p s j -> p j s"))
-        theta = coefs[:, 0, :]
-        b_t = [coefs[:, 1, :], coefs[:, 2, :]]
-        c_t = [coefs[:, 3, :], coefs[:, 4, :]]
-        turns = tables.tile([P, n_coef], F32)
-        nc.vector.tensor_scalar(out=turns[:], in0=theta, scalar1=1.0 / (2.0 * math.pi),
-                                scalar2=ROUND_MAGIC, op0=ALU.mult, op1=ALU.add)
-        nc.vector.tensor_scalar(out=turns[:], in0=turns[:], scalar1=ROUND_MAGIC, scalar2=None,
-                                op0=ALU.subtract)
-        reduced = tables.tile([P, n_coef], F32)
-        nc.vector.scalar_tensor_tensor(out=reduced[:], in0=turns[:], scalar=-TWO_PI_HI,
-                                       in1=theta, op0=ALU.mult, op1=ALU.add)
-        nc.vector.scalar_tensor_tensor(out=reduced[:], in0=turns[:], scalar=-TWO_PI_MID,
-                                       in1=reduced[:], op0=ALU.mult, op1=ALU.add)
-        nc.vector.scalar_tensor_tensor(out=reduced[:], in0=turns[:], scalar=-TWO_PI_LO,
-                                       in1=reduced[:], op0=ALU.mult, op1=ALU.add)
-        nc.vector.tensor_scalar(out=reduced[:], in0=reduced[:], scalar1=PI_BELOW,
-                                scalar2=-PI_BELOW, op0=ALU.min, op1=ALU.max)
-        sin_t = tables.tile([P, n_coef], F32)
-        nc.scalar.activation(out=sin_t[:], in_=reduced[:], func=ACT.Sin)
-        half = tables.tile([P, n_coef], F32)
-        nc.scalar.activation(out=half[:], in_=reduced[:], func=ACT.Sin, scale=0.5)
-        nc.scalar.activation(out=half[:], in_=half[:], func=ACT.Square, scale=math.sqrt(2.0))
-        cos_t = tables.tile([P, n_coef], F32)
-        nc.vector.tensor_scalar(out=cos_t[:], in0=half[:], scalar1=-1.0, scalar2=1.0,
-                                op0=ALU.mult, op1=ALU.add)
-        neg_sin_t = tables.tile([P, n_coef], F32)
-        nc.vector.tensor_scalar(out=neg_sin_t[:], in0=sin_t[:], scalar1=-1.0, scalar2=None,
-                                op0=ALU.mult)
+        ctx.enter_context(tc.manual_schedule(engines={
+            mybir.EngineType.PE, mybir.EngineType.Activation, mybir.EngineType.DVE,
+            mybir.EngineType.Pool}))
 
-        x_bank = transpose_word_blocks(nc, psum_out, ident_f32, x_sb[:])
-        x_grouped = mxops.tile([P, 2, P, 4], BF16, align_bytes=64)
-        nc.scalar.copy(out=x_grouped[:].bitcast(F32),
-                       in_=x_bank[:].rearrange("p (a u) n -> p a n u", u=2))
+        norm_w_all = consts.tile([P, D], BF16)
+
+        w_in_rows, w_out_rows, rows = {}, {}, {}
+        for k in range(5):
+            w_in_rows[k] = load_w_in(k)
+            if k < 4:
+                rows[k] = load_state(k)
+            if k == 3:
+                w_out_rows[0] = load_w_out(0)
+
         x_codes = mxops.tile([P, 2 * P], U32, align_bytes=64)
         x_scales = mxops.tile([P, 2 * P], U8, align_bytes=64)
-        nc.vector.quantize_mx(out=x_codes[:].bitcast(FP8X4), scales=x_scales[:],
-                              in_=x_grouped[:].rearrange("p a n j -> p (a n j)"))
-
         xin_t = mid.tile([P, N_TILES, P], F32)
 
         def group_words(bank, tag):
@@ -164,105 +146,111 @@ def tile_recursivemamba130m_kernel(
                                     start=(a == 0), stop=(a == 1))
             return xin_bank
 
-        wo_codes = mxops.tile([P, 8, 4 * P], U32, align_bytes=64)
-        wo_scales = mxops.tile([P, 8, 4 * P], U8, align_bytes=64)
+        wo_codes = mxops.tile([P, 4, D], U32, align_bytes=64)
+        wo_scales = mxops.tile([P, 4, D], U8, align_bytes=64)
 
-        def quantise_w_out(r, half_k, wo_grouped):
-            words = slice(half_k * 2 * P, (half_k + 1) * 2 * P)
-            nc.vector.quantize_mx(out=wo_codes[:, r, words].bitcast(FP8X4),
-                                  scales=wo_scales[:, r, words],
-                                  in_=wo_grouped[:].rearrange("p c n q -> p (c n q)"))
+        def group_w_out(bank):
+            grouped = wgroup.tile([P, 2 * P, 4], BF16, tag="w_out_grouped", align_bytes=64)
+            nc.scalar.copy(out=grouped[:].bitcast(F32), in_=bank[:].rearrange("p u r n -> p (r n) u"))
+            return grouped
+
+        def quantise_w_out(pair, c, grouped):
+            rows_n = slice(pair * 2 * P, (pair + 1) * 2 * P)
+            nc.vector.quantize_mx(out=wo_codes[:, c, rows_n].bitcast(FP8X4),
+                                  scales=wo_scales[:, c, rows_n],
+                                  in_=grouped[:].rearrange("p n j -> p (n j)"))
+
+        def multiply_y(c, o_banks):
+            for nb in range(2):
+                rows_n = slice(nb * 512, (nb + 1) * 512)
+                nc.tensor.matmul_mx(out=o_banks[nb][:],
+                                    lhsT=y_codes[:, c * P : (c + 1) * P].bitcast(FP8X4),
+                                    lhsT_scale=y_scales[:, c * P : (c + 1) * P],
+                                    rhs=wo_codes[:, c, rows_n].bitcast(FP8X4),
+                                    rhs_scale=wo_scales[:, c, rows_n],
+                                    start=(c == 0), stop=(c == 3))
 
         y_grouped = mxops.tile([P, 4, P, 4], BF16, align_bytes=64)
         y_codes = mxops.tile([P, 4 * P], U32, align_bytes=64)
         y_scales = mxops.tile([P, 4 * P], U8, align_bytes=64)
 
         def turn_old_state(rows):
-            old_t = []
-            for h in range(2):
-                words = rows[h][:].bitcast(F32).rearrange("t (f q) -> t q f", q=4)
-                bank = psum_in.tile([P, 4, P], F32, tag="in")
-                for q in range(4):
-                    nc.tensor.transpose(bank[:, q, :], words[:, q, :], ident_f32[:])
-                old_t.append(bank[:].bitcast(BF16).rearrange("p q (t e) -> p q e t", e=2))
-            return old_t
+            banks = []
+            for half_s in range(2):
+                bank = psum_in.tile([P, 2, 2, P], F32, tag="in")
+                for h in range(2):
+                    words = rows[h][:].bitcast(F32).rearrange("t (f q) -> t q f", q=4)
+                    for q in range(2):
+                        nc.tensor.transpose(bank[:, h, q, :], words[:, 2 * half_s + q, :],
+                                            ident_f32[:])
+                banks.append(bank[:].bitcast(BF16).rearrange("p h q (t e) -> p h q e t", e=2))
+            return banks
 
-        def scale_real(k, old_t):
-            new_real_t = work.tile([P, S, P], F32, tag="new_real_t")
-            new_imag_t = work.tile([P, S, P], F32, tag="new_imag_t")
+        def slot(old_t, s):
+            return old_t[s // 4][:, :, s % 4 // 2, s % 2, :]
+
+        def scale(k, old_t):
+            sines = work.tile([P, S, 2, P], F32, tag="sines")
             for s in range(S):
                 one = slice(k * S + s, k * S + s + 1)
-                nc.scalar.activation(out=new_real_t[:, s, :], in_=old_t[0][:, s // 2, s % 2, :],
-                                     func=ACT.Copy, scale=cos_t[:, one])
-                nc.scalar.activation(out=new_imag_t[:, s, :], in_=old_t[0][:, s // 2, s % 2, :],
-                                     func=ACT.Copy, scale=sin_t[:, one])
-            return new_real_t, new_imag_t
+                for h, factor in enumerate((neg_sin_t, sin_t)):
+                    nc.scalar.activation(out=sines[:, s, h, :], in_=slot(old_t, s)[:, 1 - h, :],
+                                         func=ACT.Copy, scale=factor[:, one])
+            return sines
 
         def drive(k):
-            drive_t = [work.tile([P, S, P], F32, tag="drive_real_t", name="drive_real_t"),
-                       work.tile([P, S, P], F32, tag="drive_imag_t", name="drive_imag_t")]
+            sums = work.tile([P, S, 2, P], F32, tag="sums")
             for s in range(S):
-                one = slice(k * S + s, k * S + s + 1)
                 for h in range(2):
-                    nc.gpsimd.tensor_scalar(out=drive_t[h][:, s, :], in0=xin_t[:, k, :],
-                                            scalar1=b_t[h][:, one], scalar2=0.0,
-                                            op0=ALU.mult, op1=ALU.add)
-            return drive_t
+                    nc.gpsimd.tensor_scalar(out=sums[:, s, h, :], in0=xin_t[:, k, :],
+                                            scalar1=b_t[h][:, k * S + s : k * S + s + 1],
+                                            scalar2=0.0, op0=ALU.mult, op1=ALU.add)
+            return sums
 
-        def rotate(k, old_t, new_t):
-            y_real_part = small.tile([P, P], F32, tag="y_real_part", bufs=6)
-            y_imag_part = small.tile([P, P], F32, tag="y_imag_part", bufs=6)
-            nc.vector.tensor_scalar(out=y_real_part[:], in0=xin_t[:, k, :],
-                                    scalar1=drive_y_t[:, k : k + 1], scalar2=None, op0=ALU.mult)
-            for s in range(S):
+        def add_term(total, values, coefficient):
+            nc.vector.scalar_tensor_tensor(out=total, in0=values, scalar=coefficient, in1=total,
+                                           op0=ALU.mult, op1=ALU.add)
+
+        def rotate(k, old_t, sums, y_part, slots):
+            for s in slots:
                 one = slice(k * S + s, k * S + s + 1)
-                old_imag = old_t[1][:, s // 2, s % 2, :]
-                nc.vector.scalar_tensor_tensor(
-                    out=new_t[0][:, s, :], in0=old_imag, scalar=neg_sin_t[:, one],
-                    in1=new_t[0][:, s, :], op0=ALU.mult, op1=ALU.add)
+                add_term(sums[:, s, :, :], slot(old_t, s), cos_t[:, one])
+                add_term(y_part[:, 0, :], slot(old_t, s)[:, 0, :], y_from_real_t[:, one])
                 if s == 0:
-                    nc.vector.tensor_scalar(out=y_imag_part[:], in0=old_imag,
+                    nc.vector.tensor_scalar(out=y_part[:, 1, :], in0=slot(old_t, s)[:, 1, :],
                                             scalar1=y_from_imag_t[:, one], scalar2=None,
                                             op0=ALU.mult)
                 else:
-                    nc.vector.scalar_tensor_tensor(
-                        out=y_imag_part[:], in0=old_imag, scalar=y_from_imag_t[:, one],
-                        in1=y_imag_part[:], op0=ALU.mult, op1=ALU.add)
-                nc.vector.scalar_tensor_tensor(
-                    out=new_t[1][:, s, :], in0=old_imag, scalar=cos_t[:, one],
-                    in1=new_t[1][:, s, :], op0=ALU.mult, op1=ALU.add)
-                nc.vector.scalar_tensor_tensor(
-                    out=y_real_part[:], in0=old_t[0][:, s // 2, s % 2, :],
-                    scalar=y_from_real_t[:, one], in1=y_real_part[:], op0=ALU.mult, op1=ALU.add)
-            return y_real_part, y_imag_part
+                    add_term(y_part[:, 1, :], slot(old_t, s)[:, 1, :], y_from_imag_t[:, one])
 
-        def turn_back_and_store(k, new_t, drive_t):
+        def turn_back(sums, sines, new_rows, h, half_s, copy_out):
+            back = psum_out.tile([P, 4, P], F32, tag="out")
+            for j in range(4):
+                s = half_s * 4 + j
+                for n, part in enumerate((sines, sums)):
+                    nc.tensor.matmul(back[:, j, :], lhsT=part[:, s, h, :], rhs=ident_f32[:],
+                                     is_transpose=True, start=(n == 0), stop=(n == 1))
+            copy_out(out=new_rows[:, :, half_s * 4 : (half_s + 1) * 4],
+                     in_=back[:].rearrange("t j f -> t f j"))
+
+        def store_state(k, h, new_rows):
+            nc.sync.dma_start(out=state_out[h][:, k * COLS : (k + 1) * COLS],
+                              in_=new_rows[:].rearrange("t f s -> t (f s)"))
+
+        def round_y(k):
+            y_back = psum_out.tile([P, P], F32, tag="out")
             for h in range(2):
-                new_rows = leave.tile([P, P, S], F32, tag="new_rows%d" % h)
-                for half_s in range(2):
-                    back = psum_out.tile([P, 4, P], F32, tag="out")
-                    for j in range(4):
-                        s = half_s * 4 + j
-                        nc.tensor.matmul(back[:, j, :], lhsT=new_t[h][:, s, :], rhs=ident_f32[:],
-                                         is_transpose=True, start=True, stop=False)
-                        nc.tensor.matmul(back[:, j, :], lhsT=drive_t[h][:, s, :], rhs=ident_f32[:],
-                                         is_transpose=True, start=False, stop=True)
-                    nc.scalar.copy(out=new_rows[:, :, half_s * 4 : (half_s + 1) * 4],
-                                   in_=back[:].rearrange("t j f -> t f j"))
-                nc.sync.dma_start(out=state_out[h][:, k * COLS : (k + 1) * COLS],
-                                  in_=new_rows[:].rearrange("t f s -> t (f s)"))
+                nc.tensor.matmul(y_back[:], lhsT=y_parts[k][:, h, :], rhs=ident_f32[:],
+                                 is_transpose=True, start=(h == 0), stop=(h == 1))
+            if k % 4 == 0:
+                y_rows[k // 4] = small.tile([P, 512], BF16, name="y_rows")
+            nc.scalar.copy(out=y_rows[k // 4][:, (k % 4) * P : (k % 4 + 1) * P], in_=y_back[:])
 
-        def round_y(y_parts):
-            y_back = psum_out.tile([P, 4, P], F32, tag="out")
-            for q in range(4):
-                real_part, imag_part = y_parts[q]
-                nc.tensor.matmul(y_back[:, q, :], lhsT=real_part[:], rhs=ident_f32[:],
-                                 is_transpose=True, start=True, stop=False)
-                nc.tensor.matmul(y_back[:, q, :], lhsT=imag_part[:], rhs=ident_f32[:],
-                                 is_transpose=True, start=False, stop=True)
-            y_rows = small.tile([P, 512], BF16, tag="y_rows")
-            nc.scalar.copy(out=y_rows[:], in_=y_back[:].rearrange("t q f -> t (q f)"))
-            return y_rows
+        def take_x_in(k):
+            nc.scalar.copy(out=xin_t[:, k, :], in_=xin_bank[k][:])
+            y_parts[k] = small.tile([P, 2, P], F32, name="y_part", bufs=8)
+            nc.scalar.activation(out=y_parts[k][:, 0, :], in_=xin_bank[k][:], func=ACT.Copy,
+                                 scale=drive_y_t[:, k : k + 1])
 
         def group_y(c, y_rows):
             y_words = y_rows[:].bitcast(F32)
@@ -277,6 +265,61 @@ def tile_recursivemamba130m_kernel(
                                   scales=y_scales[:, c * P : (c + 1) * P],
                                   in_=y_grouped[:, c, :, :].rearrange("p t q -> p (t q)"))
 
+        xin_bank, old, sines, sums, y_parts, y_rows = {}, {}, {}, {}, {}, {}
+        o_banks = []
+
+        sin_touch = small.tile([P, 1], F32)
+        nc.vector.memset(sin_touch[:], 0.0)
+        nc.scalar.activation(out=sin_touch[:], in_=sin_touch[:], func=ACT.Sin)
+        n_coef = N_TILES * S
+        coef_bank = psum_in.tile([P, S, P], BF16, tag="in")
+        for s in range(S):
+            nc.tensor.transpose(coef_bank[:, s, :], coef_rows[:, s : COLS : S], ident_bf16[:])
+        coefs = tables.tile([P, 5, n_coef], F32)
+        nc.scalar.copy(out=coefs[:].rearrange("p i (k s) -> p (i k) s", s=S),
+                       in_=coef_bank[:, :, 0 : 5 * N_TILES].rearrange("p s j -> p j s"))
+        theta = coefs[:, 0, :]
+        b_t = [coefs[:, 1, :], coefs[:, 2, :]]
+        c_t = [coefs[:, 3, :], coefs[:, 4, :]]
+        x_bank = transpose_word_blocks(nc, psum_out, ident_f32, x_sb[:])
+        x_grouped = mxops.tile([P, 2, P, 4], BF16, align_bytes=64)
+        nc.scalar.copy(out=x_grouped[:].bitcast(F32),
+                       in_=x_bank[:].rearrange("p (a u) n -> p a n u", u=2))
+        w_grouped = group_words(transpose_word_blocks(nc, psum_out, ident_f32, w_in_rows[0][:]),
+                                "w_in_grouped")
+        old[0] = turn_old_state(rows[0])
+        turns = tables.tile([P, n_coef], F32)
+        nc.vector.tensor_scalar(out=turns[:], in0=theta, scalar1=1.0 / (2.0 * math.pi),
+                                scalar2=ROUND_MAGIC, op0=ALU.mult, op1=ALU.add)
+        nc.vector.tensor_scalar(out=turns[:], in0=turns[:], scalar1=ROUND_MAGIC, scalar2=None,
+                                op0=ALU.subtract)
+        reduced = tables.tile([P, n_coef], F32)
+        nc.vector.scalar_tensor_tensor(out=reduced[:], in0=turns[:], scalar=-TWO_PI_HI,
+                                       in1=theta, op0=ALU.mult, op1=ALU.add)
+        nc.vector.scalar_tensor_tensor(out=reduced[:], in0=turns[:], scalar=-TWO_PI_MID,
+                                       in1=reduced[:], op0=ALU.mult, op1=ALU.add)
+        nc.vector.scalar_tensor_tensor(out=reduced[:], in0=turns[:], scalar=-TWO_PI_LO,
+                                       in1=reduced[:], op0=ALU.mult, op1=ALU.add)
+        nc.vector.tensor_scalar(out=reduced[:], in0=reduced[:], scalar1=PI_BELOW,
+                                scalar2=-PI_BELOW, op0=ALU.min, op1=ALU.max)
+        sin_t = tables.tile([P, n_coef], F32)
+        nc.scalar.activation(out=sin_t[:], in_=reduced[:], func=ACT.Sin)
+        half = tables.tile([P, n_coef], F32)
+        nc.scalar.activation(out=half[:], in_=reduced[:], func=ACT.Sin, scale=0.5)
+        nc.scalar.activation(out=half[:], in_=half[:], func=ACT.Square, scale=math.sqrt(2.0))
+        nc.vector.quantize_mx(out=x_codes[:].bitcast(FP8X4), scales=x_scales[:],
+                              in_=x_grouped[:].rearrange("p a n j -> p (a n j)"))
+
+        xin_bank[0] = multiply_x(*quantise_w_in(w_grouped))
+        cos_t = tables.tile([P, n_coef], F32)
+        nc.vector.tensor_scalar(out=cos_t[:], in0=half[:], scalar1=-1.0, scalar2=1.0,
+                                op0=ALU.mult, op1=ALU.add)
+        neg_sin_t = tables.tile([P, n_coef], F32)
+        nc.vector.tensor_scalar(out=neg_sin_t[:], in0=sin_t[:], scalar1=-1.0, scalar2=None,
+                                op0=ALU.mult)
+
+        sines[0] = scale(0, old[0])
+
         def combine(name, first, first_sign, second, second_sign, with_first, with_second):
             part = tables.tile([P, n_coef], F32, tag="part", bufs=2)
             total = tables.tile([P, n_coef], F32, name=name)
@@ -287,6 +330,10 @@ def tile_recursivemamba130m_kernel(
             nc.vector.tensor_tensor(out=total[:], in0=total[:], in1=part[:], op=ALU.add)
             return total
 
+        neg_c_imag_t = tables.tile([P, n_coef], F32)
+        nc.vector.tensor_scalar(out=neg_c_imag_t[:], in0=c_t[1], scalar1=-1.0, scalar2=None,
+                                op0=ALU.mult)
+        y_from_new = [c_t[0], neg_c_imag_t]
         y_from_imag_t = combine("y_from_imag_t", c_t[0], -1.0, c_t[1], -1.0, sin_t[:], cos_t[:])
         y_from_real_t = combine("y_from_real_t", c_t[0], 1.0, c_t[1], -1.0, cos_t[:], sin_t[:])
         y_from_drive = combine("y_from_drive", c_t[0], 1.0, c_t[1], -1.0, b_t[0], b_t[1])
@@ -294,98 +341,115 @@ def tile_recursivemamba130m_kernel(
         nc.vector.tensor_reduce(out=drive_y_t[:],
                                 in_=y_from_drive[:].rearrange("p (k s) -> p k s", s=S),
                                 axis=AX.X, op=ALU.add)
-        norm_w_all = consts.tile([P, D], BF16)
+        take_x_in(0)
+        sums[0] = drive(0)
+        rotate(0, old[0], sums[0], y_parts[0], range(4))
 
-        w_in_rows, w_out_rows, rows = {}, {}, {}
-        for k in range(3):
-            w_in_rows[k] = load_w_in(k)
-            rows[k] = load_state(k)
-        w_out_rows[0] = load_w_out(0)
+        for k in range(1, 3):
+            xin_bank[k] = multiply_x(*quantise_w_in(group_words(
+                transpose_word_blocks(nc, psum_out, ident_f32, w_in_rows[k][:]), "w_in_grouped")))
+        take_x_in(1)
+        w_bank = [transpose_word_blocks(nc, psum_out, ident_f32, w_in_rows[3][:]),
+                  transpose_w_out_words(nc, psum_out, ident_f32, w_out_rows[0], 0)]
 
-        w_grouped, wo_grouped, w_quant = {}, {}, {}
-        xin_bank, old, scaled, driven, y_parts, y_rows = {}, {}, {}, {}, {}, {}
-        ordered = (mybir.EngineType.PE, mybir.EngineType.Activation, mybir.EngineType.DVE,
-                   mybir.EngineType.Pool)
-        with tc.manual_schedule(engines=set(ordered)):
-            for i in range(-4, N_TILES + 3):
-                if 3 <= i + 4 < N_TILES:
-                    rows[i + 4] = load_state(i + 4)
-                if 3 <= i + 7 < N_TILES:
-                    w_in_rows[i + 7] = load_w_in(i + 7)
-                if i >= 0 and i % 2 == 0 and i // 2 + 1 < S:
-                    w_out_rows[i // 2 + 1] = load_w_out(i // 2 + 1)
-                if i == 10:
-                    nc.sync.dma_start(out=norm_w_all[:], in_=norm_w.partition_broadcast(P))
+        for i in range(N_TILES):
+            if i + 4 < N_TILES:
+                rows[i + 4] = load_state(i + 4)
+            if i + 5 < N_TILES:
+                w_in_rows[i + 5] = load_w_in(i + 5)
+            if i % 4 == 0 and i // 4 + 1 < 4:
+                w_out_rows[i // 4 + 1] = load_w_out(i // 4 + 1)
+            if i == 10:
+                nc.sync.dma_start(out=norm_w_all[:], in_=norm_w.partition_broadcast(P))
 
-                if i + 4 < N_TILES:
-                    w_bank = transpose_word_blocks(nc, psum_out, ident_f32, w_in_rows[i + 4][:])
-                if 0 <= i < N_TILES:
-                    wo_bank = transpose_word_blocks(
-                        nc, psum_out, ident_f32,
-                        w_out_rows[i // 2][:, (i % 2) * D : (i % 2 + 1) * D])
-                if 0 <= i + 2 < N_TILES:
-                    nc.scalar.copy(out=xin_t[:, i + 2, :], in_=xin_bank[i + 2][:])
-                if i + 4 < N_TILES:
-                    w_grouped[i + 4] = group_words(w_bank, "w_in_grouped")
-                if 0 <= i < N_TILES:
-                    wo_grouped[i] = group_words(wo_bank, "w_out_grouped")
-                if 0 <= i + 1 < N_TILES:
-                    old[i + 1] = turn_old_state(rows[i + 1])
-                if 0 <= i + 3 < N_TILES:
-                    w_quant[i + 3] = quantise_w_in(w_grouped[i + 3])
-                if 0 <= i - 1 < N_TILES:
-                    quantise_w_out((i - 1) // 2, (i - 1) % 2, wo_grouped[i - 1])
-                if i >= 6 and i % 4 == 2:
-                    quantise_y(i // 4 - 1)
-                if 0 <= i + 1 < N_TILES:
-                    driven[i + 1] = drive(i + 1)
-                if 0 <= i - 1 < N_TILES:
-                    turn_back_and_store(i - 1, scaled[i - 1], driven[i - 1])
-                if i >= 4 and i % 4 == 0:
-                    y_rows[i // 4 - 1] = round_y(y_parts)
-                if i >= 5 and i % 4 == 1:
-                    group_y(i // 4 - 1, y_rows[i // 4 - 1])
-                if 0 <= i + 3 < N_TILES:
-                    xin_bank[i + 3] = multiply_x(*w_quant[i + 3])
-                if 0 <= i + 1 < N_TILES:
-                    scaled[i + 1] = scale_real(i + 1, old[i + 1])
-                if 0 <= i < N_TILES:
-                    y_parts[i % 4] = rotate(i, old[i], scaled[i])
+            if i + 3 < N_TILES:
+                w_grouped = group_words(w_bank[0], "w_in_grouped")
+            wo_grouped = group_w_out(w_bank[1])
+            if i + 2 < N_TILES:
+                take_x_in(i + 2)
+            if i + 1 < N_TILES:
+                old[i + 1] = turn_old_state(rows[i + 1])
+            if i == N_TILES - 1:
+                for nb in range(2):
+                    o_bank = psum_in.tile([P, 512], F32, tag="in")
+                    o_banks.append(o_bank)
+                for c in range(2):
+                    multiply_y(c, o_banks)
+            if i >= 1:
+                rotate(i, old[i], sums[i], y_parts[i], range(4))
+            if i + 1 < N_TILES:
+                sines[i + 1] = scale(i + 1, old[i + 1])
+            if i + 1 < N_TILES:
+                sums[i + 1] = drive(i + 1)
+            if i >= 1:
+                new_rows = leave.tile([P, P, S], F32, tag="new_rows0", name="new_rows0")
+                for half_s in range(2):
+                    turn_back(sums[i - 1], sines[i - 1], new_rows, 0, half_s, nc.scalar.copy)
+                store_state(i - 1, 0, new_rows)
+                new_rows = leave.tile([P, P, S], F32, tag="new_rows1", name="new_rows1")
+                turn_back(sums[i - 1], sines[i - 1], new_rows, 1, 0, nc.scalar.copy)
+            if i >= 1:
+                turn_back(sums[i - 1], sines[i - 1], new_rows, 1, 1, nc.scalar.copy)
+                store_state(i - 1, 1, new_rows)
+            rotate(i, old[i], sums[i], y_parts[i], range(4, 6))
+            if i + 3 < N_TILES:
+                w_quant = quantise_w_in(w_grouped)
+            quantise_w_out(i // 4, i % 4, wo_grouped)
+            if i >= 6 and i % 4 == 2:
+                quantise_y(i // 4 - 1)
+            rotate(i, old[i], sums[i], y_parts[i], range(6, S))
+            if i >= 1:
+                round_y(i - 1)
+            if i >= 5 and i % 4 == 1:
+                group_y(i // 4 - 1, y_rows[i // 4 - 1])
+            if i + 4 < N_TILES:
+                w_bank[0] = transpose_word_blocks(nc, psum_out, ident_f32, w_in_rows[i + 4][:])
+            if i + 1 < N_TILES:
+                w_bank[1] = transpose_w_out_words(nc, psum_out, ident_f32,
+                                                  w_out_rows[(i + 1) // 4], (i + 1) % 4)
+            if i + 3 < N_TILES:
+                xin_bank[i + 3] = multiply_x(*w_quant)
 
-        o_banks = []
+        multiply_y(2, o_banks)
+
+        k = N_TILES - 1
+        table_touch = small.tile([P, 1], F32)
+        nc.vector.tensor_scalar(out=table_touch[:], in0=y_parts[k - 1][:, 0, 0:1], scalar1=0.0,
+                                scalar2=1.0, op0=ALU.mult, op1=ALU.add)
+        nc.scalar.activation(out=table_touch[:], in_=table_touch[:], func=ACT.Abs_reciprocal_sqrt)
+        last_rows = [leave.tile([P, P, S], F32, tag="new_rows0", name="new_rows0"),
+                     leave.tile([P, P, S], F32, tag="new_rows1", name="new_rows1")]
+        round_y(k)
+        turn_back(sums[k], sines[k], last_rows[0], 0, 0, nc.vector.tensor_copy)
+        turn_back(sums[k], sines[k], last_rows[0], 0, 1, nc.vector.tensor_copy)
+        group_y(3, y_rows[3])
+        quantise_y(3)
+        store_state(k, 0, last_rows[0])
+        turn_back(sums[k], sines[k], last_rows[1], 1, 0, nc.vector.tensor_copy)
+        multiply_y(3, o_banks)
+
+        square_sums = small.tile([P, 2], F32)
+        gained = mid.tile([P, D], F32)
         for nb in range(2):
-            o_bank = psum_in.tile([P, 4, P], F32, tag="in")
-            o_banks.append(o_bank)
-            for i in range(4):
-                for c in range(4):
-                    cols = slice(c * P, (c + 1) * P)
-                    nc.tensor.matmul_mx(out=o_bank[:, i, :],
-                                        lhsT=y_codes[:, cols].bitcast(FP8X4),
-                                        lhsT_scale=y_scales[:, cols],
-                                        rhs=wo_codes[:, nb * 4 + i, cols].bitcast(FP8X4),
-                                        rhs_scale=wo_scales[:, nb * 4 + i, cols],
-                                        start=(c == 0), stop=(c == 3))
-
-        sums = small.tile([P, 2], F32)
-        for nb in range(2):
+            cols = slice((1 - nb) * 512, (2 - nb) * 512)
             squares = small.tile([P, 512], F32, tag="squares")
-            nc.scalar.activation(out=squares[:], in_=o_banks[nb][:].rearrange("p i n -> p (i n)"),
-                                 func=ACT.Square, accum_out=sums[:, nb : nb + 1])
-        mean_sq = small.tile([P, 1], F32)
-        nc.vector.tensor_tensor(out=mean_sq[:], in0=sums[:, 0:1], in1=sums[:, 1:2], op=ALU.add)
-        nc.vector.tensor_scalar(out=mean_sq[:], in0=mean_sq[:], scalar1=1.0 / D, scalar2=EPS,
-                                op0=ALU.mult, op1=ALU.add)
-        rms = small.tile([P, 1], F32)
-        nc.scalar.activation(out=rms[:], in_=mean_sq[:], func=ACT.Sqrt)
+            nc.scalar.activation(out=squares[:], in_=o_banks[nb][:], func=ACT.Square,
+                                 accum_out=square_sums[:, nb : nb + 1])
+            nc.vector.tensor_tensor(out=gained[:, cols], in0=o_banks[1 - nb][:],
+                                    in1=norm_w_all[:, cols], op=ALU.mult)
+        total = small.tile([P, 1], F32)
+        nc.vector.tensor_scalar(out=total[:], in0=square_sums[:, 0:1], scalar1=square_sums[:, 1:2],
+                                scalar2=D * EPS, op0=ALU.add, op1=ALU.add)
         inv_rms = small.tile([P, 1], F32)
-        nc.vector.reciprocal(out=inv_rms[:], in_=rms[:])
+        nc.scalar.activation(out=inv_rms[:], in_=total[:], func=ACT.Abs_reciprocal_sqrt,
+                             scale=1.0 / D)
+        turn_back(sums[k], sines[k], last_rows[1], 1, 1, nc.scalar.copy)
+        store_state(k, 1, last_rows[1])
         result = mid.tile([P, D], F32)
         for nb in range(2):
             cols = slice(nb * 512, (nb + 1) * 512)
-            nc.vector.scalar_tensor_tensor(out=result[:, cols],
-                                           in0=o_banks[nb][:].rearrange("p i n -> p (i n)"),
-                                           scalar=inv_rms[:, 0:1], in1=norm_w_all[:, cols],
-                                           op0=ALU.mult, op1=ALU.mult)
-            nc.vector.tensor_tensor(out=result[:, cols], in0=result[:, cols], in1=x_sb[:, cols],
-                                    op=ALU.add)
-        nc.sync.dma_start(out=out_0.rearrange("b l d -> (b l) d"), in_=result[:])
+            nc.vector.scalar_tensor_tensor(out=result[:, cols], in0=gained[:, cols],
+                                           scalar=inv_rms[:, 0:1], in1=x_sb[:, cols],
+                                           op0=ALU.mult, op1=ALU.add)
+            nc.sync.dma_start(out=out_0.rearrange("b l d -> (b l) d")[:, cols],
+                              in_=result[:, cols])

@@ -189,32 +189,37 @@ def tile_recursivemamba130m_kernel(
         def slot(old_t, s):
             return old_t[s // 4][:, :, s % 4 // 2, s % 2, :]
 
-        def scale(k, old_t):
-            sines = work.tile([P, S, 2, P], F32, tag="sines")
-            for s in range(S):
+        def scale(k, old_t, slots=range(S)):
+            if 0 in slots:
+                sines[k] = work.tile([P, S, 2, P], F32, tag="sines", name="sines")
+            for s in slots:
                 one = slice(k * S + s, k * S + s + 1)
                 for h, factor in enumerate((neg_sin_t, sin_t)):
-                    nc.scalar.activation(out=sines[:, s, h, :], in_=slot(old_t, s)[:, 1 - h, :],
+                    nc.scalar.activation(out=sines[k][:, s, h, :], in_=slot(old_t, s)[:, 1 - h, :],
                                          func=ACT.Copy, scale=factor[:, one])
-            return sines
 
         def drive(k):
             sums = work.tile([P, S, 2, P], F32, tag="sums")
-            for s in range(S):
-                for h in range(2):
-                    nc.gpsimd.tensor_scalar(out=sums[:, s, h, :], in0=xin_t[:, k, :],
-                                            scalar1=b_t[h][:, k * S + s : k * S + s + 1],
-                                            scalar2=0.0, op0=ALU.mult, op1=ALU.add)
+            for s in range(0, S, 4):
+                b_slots = coefs[:, 1:3, k * S + s : k * S + s + 4].rearrange("p h s -> p s h")
+                nc.gpsimd.tensor_tensor(
+                    out=sums[:, s : s + 4, :, :],
+                    in0=xin_t[:, k, :].unsqueeze(1).unsqueeze(1).to_broadcast([P, 4, 2, P]),
+                    in1=b_slots.unsqueeze(3).to_broadcast([P, 4, 2, P]), op=ALU.mult)
             return sums
 
         def add_term(total, values, coefficient):
             nc.vector.scalar_tensor_tensor(out=total, in0=values, scalar=coefficient, in1=total,
                                            op0=ALU.mult, op1=ALU.add)
 
-        def rotate(k, old_t, sums, y_part, slots):
+        def add_cosines(k, slots):
+            for s in slots:
+                add_term(sums[k][:, s, :, :], slot(old[k], s), cos_t[:, k * S + s : k * S + s + 1])
+
+        def add_to_y(k, slots):
+            old_t, y_part = old[k], y_parts[k]
             for s in slots:
                 one = slice(k * S + s, k * S + s + 1)
-                add_term(sums[:, s, :, :], slot(old_t, s), cos_t[:, one])
                 add_term(y_part[:, 0, :], slot(old_t, s)[:, 0, :], y_from_real_t[:, one])
                 if s == 0:
                     nc.vector.tensor_scalar(out=y_part[:, 1, :], in0=slot(old_t, s)[:, 1, :],
@@ -223,13 +228,22 @@ def tile_recursivemamba130m_kernel(
                 else:
                     add_term(y_part[:, 1, :], slot(old_t, s)[:, 1, :], y_from_imag_t[:, one])
 
-        def turn_back(sums, sines, new_rows, h, half_s, copy_out):
+        def add_sines(k, h):
+            nc.vector.tensor_tensor(out=sums[k][:, :, h, :], in0=sums[k][:, :, h, :],
+                                    in1=sines[k][:, :, h, :], op=ALU.add)
+
+        def rotate(k, slots):
+            for s in slots:
+                add_cosines(k, [s])
+                add_to_y(k, [s])
+
+        def turn_back(parts, new_rows, h, half_s, copy_out):
             back = psum_out.tile([P, 4, P], F32, tag="out")
             for j in range(4):
                 s = half_s * 4 + j
-                for n, part in enumerate((sines, sums)):
+                for n, part in enumerate(parts):
                     nc.tensor.matmul(back[:, j, :], lhsT=part[:, s, h, :], rhs=ident_f32[:],
-                                     is_transpose=True, start=(n == 0), stop=(n == 1))
+                                     is_transpose=True, start=(n == 0), stop=(n == len(parts) - 1))
             copy_out(out=new_rows[:, :, half_s * 4 : (half_s + 1) * 4],
                      in_=back[:].rearrange("t j f -> t f j"))
 
@@ -248,9 +262,12 @@ def tile_recursivemamba130m_kernel(
 
         def take_x_in(k):
             nc.scalar.copy(out=xin_t[:, k, :], in_=xin_bank[k][:])
-            y_parts[k] = small.tile([P, 2, P], F32, name="y_part", bufs=8)
-            nc.scalar.activation(out=y_parts[k][:, 0, :], in_=xin_bank[k][:], func=ACT.Copy,
-                                 scale=drive_y_t[:, k : k + 1])
+
+        def start_y(k):
+            y_parts[k] = small.tile([P, 2, P], F32, name="y_part", bufs=4)
+            nc.gpsimd.tensor_scalar(out=y_parts[k][:, 0, :], in0=xin_t[:, k, :],
+                                    scalar1=drive_y_t[:, k : k + 1], scalar2=0.0,
+                                    op0=ALU.mult, op1=ALU.add)
 
         def group_y(c, y_rows):
             y_words = y_rows[:].bitcast(F32)
@@ -270,6 +287,8 @@ def tile_recursivemamba130m_kernel(
 
         sin_touch = small.tile([P, 1], F32)
         nc.vector.memset(sin_touch[:], 0.0)
+        root_touch = small.tile([P, 1], F32)
+        nc.vector.memset(root_touch[:], 1.0)
         nc.scalar.activation(out=sin_touch[:], in_=sin_touch[:], func=ACT.Sin)
         n_coef = N_TILES * S
         coef_bank = psum_in.tile([P, S, P], BF16, tag="in")
@@ -311,6 +330,8 @@ def tile_recursivemamba130m_kernel(
                               in_=x_grouped[:].rearrange("p a n j -> p (a n j)"))
 
         xin_bank[0] = multiply_x(*quantise_w_in(w_grouped))
+        take_x_in(0)
+        sums[0] = drive(0)
         cos_t = tables.tile([P, n_coef], F32)
         nc.vector.tensor_scalar(out=cos_t[:], in0=half[:], scalar1=-1.0, scalar2=1.0,
                                 op0=ALU.mult, op1=ALU.add)
@@ -318,7 +339,9 @@ def tile_recursivemamba130m_kernel(
         nc.vector.tensor_scalar(out=neg_sin_t[:], in0=sin_t[:], scalar1=-1.0, scalar2=None,
                                 op0=ALU.mult)
 
-        sines[0] = scale(0, old[0])
+        w_grouped = group_words(transpose_word_blocks(nc, psum_out, ident_f32, w_in_rows[1][:]),
+                                "w_in_grouped")
+        scale(0, old[0], range(4))
 
         def combine(name, first, first_sign, second, second_sign, with_first, with_second):
             part = tables.tile([P, n_coef], F32, tag="part", bufs=2)
@@ -330,10 +353,6 @@ def tile_recursivemamba130m_kernel(
             nc.vector.tensor_tensor(out=total[:], in0=total[:], in1=part[:], op=ALU.add)
             return total
 
-        neg_c_imag_t = tables.tile([P, n_coef], F32)
-        nc.vector.tensor_scalar(out=neg_c_imag_t[:], in0=c_t[1], scalar1=-1.0, scalar2=None,
-                                op0=ALU.mult)
-        y_from_new = [c_t[0], neg_c_imag_t]
         y_from_imag_t = combine("y_from_imag_t", c_t[0], -1.0, c_t[1], -1.0, sin_t[:], cos_t[:])
         y_from_real_t = combine("y_from_real_t", c_t[0], 1.0, c_t[1], -1.0, cos_t[:], sin_t[:])
         y_from_drive = combine("y_from_drive", c_t[0], 1.0, c_t[1], -1.0, b_t[0], b_t[1])
@@ -341,18 +360,25 @@ def tile_recursivemamba130m_kernel(
         nc.vector.tensor_reduce(out=drive_y_t[:],
                                 in_=y_from_drive[:].rearrange("p (k s) -> p k s", s=S),
                                 axis=AX.X, op=ALU.add)
-        take_x_in(0)
-        sums[0] = drive(0)
-        rotate(0, old[0], sums[0], y_parts[0], range(4))
-
-        for k in range(1, 3):
-            xin_bank[k] = multiply_x(*quantise_w_in(group_words(
-                transpose_word_blocks(nc, psum_out, ident_f32, w_in_rows[k][:]), "w_in_grouped")))
+        y_parts[0] = small.tile([P, 2, P], F32, name="y_part", bufs=4)
+        nc.scalar.activation(out=y_parts[0][:, 0, :], in_=xin_t[:, 0, :], func=ACT.Copy,
+                             scale=drive_y_t[:, 0:1])
+        xin_bank[1] = multiply_x(*quantise_w_in(w_grouped))
+        w_bank = transpose_word_blocks(nc, psum_out, ident_f32, w_in_rows[2][:])
         take_x_in(1)
+        scale(0, old[0], range(4, 6))
+        w_grouped = group_words(w_bank, "w_in_grouped")
+        scale(0, old[0], range(6, S))
+        nc.scalar.activation(out=root_touch[:], in_=root_touch[:], func=ACT.Abs_reciprocal_sqrt)
+        rotate(0, range(3))
+        old[1] = turn_old_state(rows[1])
+        xin_bank[2] = multiply_x(*quantise_w_in(w_grouped))
+        rotate(0, range(3, 4))
         w_bank = [transpose_word_blocks(nc, psum_out, ident_f32, w_in_rows[3][:]),
                   transpose_w_out_words(nc, psum_out, ident_f32, w_out_rows[0], 0)]
 
-        for i in range(N_TILES):
+        k = N_TILES - 1
+        for i in range(k):
             if i + 4 < N_TILES:
                 rows[i + 4] = load_state(i + 4)
             if i + 5 < N_TILES:
@@ -367,37 +393,32 @@ def tile_recursivemamba130m_kernel(
             wo_grouped = group_w_out(w_bank[1])
             if i + 2 < N_TILES:
                 take_x_in(i + 2)
-            if i + 1 < N_TILES:
+            if 1 <= i < N_TILES - 1:
                 old[i + 1] = turn_old_state(rows[i + 1])
-            if i == N_TILES - 1:
-                for nb in range(2):
-                    o_bank = psum_in.tile([P, 512], F32, tag="in")
-                    o_banks.append(o_bank)
-                for c in range(2):
-                    multiply_y(c, o_banks)
             if i >= 1:
-                rotate(i, old[i], sums[i], y_parts[i], range(4))
+                rotate(i, range(4))
             if i + 1 < N_TILES:
-                sines[i + 1] = scale(i + 1, old[i + 1])
+                scale(i + 1, old[i + 1])
             if i + 1 < N_TILES:
+                start_y(i + 1)
                 sums[i + 1] = drive(i + 1)
             if i >= 1:
                 new_rows = leave.tile([P, P, S], F32, tag="new_rows0", name="new_rows0")
                 for half_s in range(2):
-                    turn_back(sums[i - 1], sines[i - 1], new_rows, 0, half_s, nc.scalar.copy)
+                    turn_back((sines[i - 1], sums[i - 1]), new_rows, 0, half_s, nc.scalar.copy)
                 store_state(i - 1, 0, new_rows)
                 new_rows = leave.tile([P, P, S], F32, tag="new_rows1", name="new_rows1")
-                turn_back(sums[i - 1], sines[i - 1], new_rows, 1, 0, nc.scalar.copy)
+                turn_back((sines[i - 1], sums[i - 1]), new_rows, 1, 0, nc.scalar.copy)
             if i >= 1:
-                turn_back(sums[i - 1], sines[i - 1], new_rows, 1, 1, nc.scalar.copy)
+                turn_back((sines[i - 1], sums[i - 1]), new_rows, 1, 1, nc.scalar.copy)
                 store_state(i - 1, 1, new_rows)
-            rotate(i, old[i], sums[i], y_parts[i], range(4, 6))
+            rotate(i, range(4, 6))
             if i + 3 < N_TILES:
                 w_quant = quantise_w_in(w_grouped)
             quantise_w_out(i // 4, i % 4, wo_grouped)
             if i >= 6 and i % 4 == 2:
                 quantise_y(i // 4 - 1)
-            rotate(i, old[i], sums[i], y_parts[i], range(6, S))
+            rotate(i, range(6, S))
             if i >= 1:
                 round_y(i - 1)
             if i >= 5 and i % 4 == 1:
@@ -410,46 +431,64 @@ def tile_recursivemamba130m_kernel(
             if i + 3 < N_TILES:
                 xin_bank[i + 3] = multiply_x(*w_quant)
 
-        multiply_y(2, o_banks)
-
-        k = N_TILES - 1
-        table_touch = small.tile([P, 1], F32)
-        nc.vector.tensor_scalar(out=table_touch[:], in0=y_parts[k - 1][:, 0, 0:1], scalar1=0.0,
-                                scalar2=1.0, op0=ALU.mult, op1=ALU.add)
-        nc.scalar.activation(out=table_touch[:], in_=table_touch[:], func=ACT.Abs_reciprocal_sqrt)
-        last_rows = [leave.tile([P, P, S], F32, tag="new_rows0", name="new_rows0"),
-                     leave.tile([P, P, S], F32, tag="new_rows1", name="new_rows1")]
+        before_rows = [leave.tile([P, P, S], F32, tag="new_rows%d" % h, name="new_rows%d" % h)
+                       for h in range(2)]
+        wo_grouped = group_w_out(w_bank[1])
+        add_to_y(k, range(S))
+        add_cosines(k, range(2))
+        quantise_w_out(3, 3, wo_grouped)
+        add_cosines(k, range(2, S))
+        for nb in range(2):
+            o_bank = psum_in.tile([P, 512], F32, tag="in")
+            o_banks.append(o_bank)
+        turn_back((sines[k - 1], sums[k - 1]), before_rows[0], 0, 0, nc.scalar.copy)
+        turn_back((sines[k - 1], sums[k - 1]), before_rows[0], 0, 1, nc.scalar.copy)
+        store_state(k - 1, 0, before_rows[0])
+        round_y(k - 1)
+        multiply_y(0, o_banks)
         round_y(k)
-        turn_back(sums[k], sines[k], last_rows[0], 0, 0, nc.vector.tensor_copy)
-        turn_back(sums[k], sines[k], last_rows[0], 0, 1, nc.vector.tensor_copy)
+        multiply_y(1, o_banks)
         group_y(3, y_rows[3])
+        turn_back((sines[k - 1], sums[k - 1]), before_rows[1], 1, 0, nc.scalar.copy)
         quantise_y(3)
-        store_state(k, 0, last_rows[0])
-        turn_back(sums[k], sines[k], last_rows[1], 1, 0, nc.vector.tensor_copy)
+        turn_back((sines[k - 1], sums[k - 1]), before_rows[1], 1, 1, nc.vector.tensor_copy)
+        store_state(k - 1, 1, before_rows[1])
+        multiply_y(2, o_banks)
         multiply_y(3, o_banks)
-
         square_sums = small.tile([P, 2], F32)
         gained = mid.tile([P, D], F32)
-        for nb in range(2):
-            cols = slice((1 - nb) * 512, (2 - nb) * 512)
-            squares = small.tile([P, 512], F32, tag="squares")
-            nc.scalar.activation(out=squares[:], in_=o_banks[nb][:], func=ACT.Square,
-                                 accum_out=square_sums[:, nb : nb + 1])
-            nc.vector.tensor_tensor(out=gained[:, cols], in0=o_banks[1 - nb][:],
-                                    in1=norm_w_all[:, cols], op=ALU.mult)
+        result = mid.tile([P, D], F32)
+        squares = small.tile([P, 512], F32, tag="squares", name="squares")
+        nc.scalar.activation(out=squares[:], in_=o_banks[0][:], func=ACT.Square,
+                             accum_out=square_sums[:, 0:1])
+        nc.vector.tensor_tensor(out=gained[:, 512:1024], in0=o_banks[1][:],
+                                in1=norm_w_all[:, 512:1024], op=ALU.mult)
+        squares = small.tile([P, 512], F32, tag="squares", name="squares")
+        nc.scalar.activation(out=squares[:], in_=o_banks[1][:], func=ACT.Square,
+                             accum_out=square_sums[:, 1:2])
+        nc.vector.tensor_tensor(out=gained[:, 0:512], in0=o_banks[0][:],
+                                in1=norm_w_all[:, 0:512], op=ALU.mult)
         total = small.tile([P, 1], F32)
         nc.vector.tensor_scalar(out=total[:], in0=square_sums[:, 0:1], scalar1=square_sums[:, 1:2],
                                 scalar2=D * EPS, op0=ALU.add, op1=ALU.add)
         inv_rms = small.tile([P, 1], F32)
         nc.scalar.activation(out=inv_rms[:], in_=total[:], func=ACT.Abs_reciprocal_sqrt,
                              scale=1.0 / D)
-        turn_back(sums[k], sines[k], last_rows[1], 1, 1, nc.scalar.copy)
+        nc.vector.scalar_tensor_tensor(out=result[:, 0:512], in0=gained[:, 0:512],
+                                       scalar=inv_rms[:, 0:1], in1=x_sb[:, 0:512],
+                                       op0=ALU.mult, op1=ALU.add)
+        nc.sync.dma_start(out=out_0.rearrange("b l d -> (b l) d")[:, 0:512],
+                          in_=result[:, 0:512])
+        nc.vector.scalar_tensor_tensor(out=result[:, 512:1024], in0=gained[:, 512:1024],
+                                       scalar=inv_rms[:, 0:1], in1=x_sb[:, 512:1024],
+                                       op0=ALU.mult, op1=ALU.add)
+        nc.sync.dma_start(out=out_0.rearrange("b l d -> (b l) d")[:, 512:1024],
+                          in_=result[:, 512:1024])
+        last_rows = [leave.tile([P, P, S], F32, tag="new_rows%d" % h, name="new_rows%d" % h)
+                     for h in range(2)]
+        turn_back((sines[k], sums[k]), last_rows[0], 0, 0, nc.scalar.copy)
+        turn_back((sines[k], sums[k]), last_rows[0], 0, 1, nc.scalar.copy)
+        store_state(k, 0, last_rows[0])
+        turn_back((sines[k], sums[k]), last_rows[1], 1, 0, nc.scalar.copy)
+        turn_back((sines[k], sums[k]), last_rows[1], 1, 1, nc.vector.tensor_copy)
         store_state(k, 1, last_rows[1])
-        result = mid.tile([P, D], F32)
-        for nb in range(2):
-            cols = slice(nb * 512, (nb + 1) * 512)
-            nc.vector.scalar_tensor_tensor(out=result[:, cols], in0=gained[:, cols],
-                                           scalar=inv_rms[:, 0:1], in1=x_sb[:, cols],
-                                           op0=ALU.mult, op1=ALU.add)
-            nc.sync.dma_start(out=out_0.rearrange("b l d -> (b l) d")[:, cols],
-                              in_=result[:, cols])

import math
from contextlib import ExitStack

import concourse.mybir as mybir
from concourse.masks import make_identity

F32 = mybir.dt.float32
BF16 = mybir.dt.bfloat16
U32 = mybir.dt.uint32
U8 = mybir.dt.uint8
FP8X4 = mybir.dt.float8_e4m3fn_x4
ALU = mybir.AluOpType
ACT = mybir.ActivationFunctionType
AX = mybir.AxisListType

P = 128
D = 1024
CD = 2048
S = 8
N_TILES = CD // P
COLS = P * S

FLOPS = 2 * P * D * CD * 2

EPS = 2.0 ** -23
ROUND_MAGIC = 12582912.0
TWO_PI_HI = 6.28125
TWO_PI_MID = 0.0019353071693331003
TWO_PI_LO = 2.0 * math.pi - TWO_PI_HI - TWO_PI_MID
PI_BELOW = 3.1415925


def transpose_word_blocks(nc, psum, ident_f32, rows_bf16):
    words = rows_bf16.bitcast(F32)
    bank = psum.tile([P, 4, P], F32, tag="out")
    for b in range(4):
        nc.tensor.transpose(bank[:, b, :], words[:, 256 * (b // 2) + b % 2 : 256 * (b // 2 + 1) : 2],
                            ident_f32[:])
    return bank


def transpose_w_out_words(nc, psum, ident_f32, pair_rows, c):
    bank = psum.tile([P, 2, 2, P], F32, tag="out")
    for r in range(2):
        words = pair_rows[:, r, c * 512 : (c + 1) * 512].bitcast(F32)
        for u in range(2):
            nc.tensor.transpose(bank[:, u, r, :], words[:, u : 256 : 2], ident_f32[:])
    return bank


def tile_recursivemamba130m_kernel(
    tc, x, real_state, imag_state, W_in, A_theta, B_real, B_imag, C_real, C_imag, W_out, norm_w,
    out_0, out_1, out_2,
):
    nc = tc.nc
    with ExitStack() as ctx:
        consts = ctx.enter_context(tc.tile_pool(name="consts", bufs=1))
        tables = ctx.enter_context(tc.tile_pool(name="tables", bufs=1))
        wstage = ctx.enter_context(tc.tile_pool(name="wstage", bufs=5))
        wgroup = ctx.enter_context(tc.tile_pool(name="wgroup", bufs=3))
        mxops = ctx.enter_context(tc.tile_pool(name="mxops", bufs=1))
        mid = ctx.enter_context(tc.tile_pool(name="mid", bufs=1))
        small = ctx.enter_context(tc.tile_pool(name="small", bufs=2))
        stage = ctx.enter_context(tc.tile_pool(name="stage", bufs=5))
        work = ctx.enter_context(tc.tile_pool(name="work", bufs=3))
        leave = ctx.enter_context(tc.tile_pool(name="leave", bufs=3))
        psum_in = ctx.enter_context(tc.psum_pool(name="psum_in", bufs=4))
        psum_out = ctx.enter_context(tc.psum_pool(name="psum_out", bufs=4))

        ident_f32 = consts.tile([P, P], F32)
        make_identity(nc, ident_f32[:])
        ident_bf16 = consts.tile([P, P], BF16)
        make_identity(nc, ident_bf16[:])

        state_in = [real_state.rearrange("b l c d s -> (b l) (c d s)"),
                    imag_state.rearrange("b l c d s -> (b l) (c d s)")]
        state_out = [out_1.rearrange("b l c d s -> (b l) (c d s)"),
                     out_2.rearrange("b l c d s -> (b l) (c d s)")]

        coef_rows = tables.tile([P, COLS], BF16)
        nc.vector.memset(coef_rows[64:P, :], 0.0)
        for i, coeff in enumerate((A_theta, B_real, B_imag, C_real, C_imag)):
            nc.sync.dma_start(out=coef_rows[i * N_TILES : (i + 1) * N_TILES, :],
                              in_=coeff.rearrange("c (k p) s -> (c k) (p s)", p=P))
        x_sb = consts.tile([P, D], BF16)
        nc.sync.dma_start(out=x_sb[:], in_=x.rearrange("b l d -> (b l) d"))

        def load_state(k):
            both = []
            for h in range(2):
                rows = stage.tile([P, COLS], BF16, tag="rows%d" % h)
                nc.sync.dma_start(out=rows[:], in_=state_in[h][:, k * COLS : (k + 1) * COLS])
                both.append(rows)
            return both

        def load_w_in(k):
            rows = wstage.tile([P, D], BF16, tag="w_in_rows")
            nc.sync.dma_start(out=rows[:], in_=W_in[k * P : (k + 1) * P, :])
            return rows

        def load_w_out(pair):
            rows = wstage.tile([P, 2, CD], BF16, tag="w_out_rows", bufs=3)
            nc.sync.dma_start(
                out=rows[:],
                in_=W_out[pair * 2 * P : (pair + 1) * 2 * P, :].rearrange("(r p) k -> p r k", p=P))
            return rows

        ctx.enter_context(tc.manual_schedule(engines={
            mybir.EngineType.PE, mybir.EngineType.Activation, mybir.EngineType.DVE,
            mybir.EngineType.Pool}))

        norm_w_all = consts.tile([P, D], BF16)

        w_in_rows, w_out_rows, rows = {}, {}, {}
        for k in range(5):
            w_in_rows[k] = load_w_in(k)
            if k < 4:
                rows[k] = load_state(k)
            if k == 3:
                w_out_rows[0] = load_w_out(0)

        x_codes = mxops.tile([P, 2 * P], U32, align_bytes=64)
        x_scales = mxops.tile([P, 2 * P], U8, align_bytes=64)
        xin_t = mid.tile([P, N_TILES, P], F32)

        def group_words(bank, tag):
            grouped = wgroup.tile([P, 2, P, 4], BF16, tag=tag, align_bytes=64)
            nc.scalar.copy(out=grouped[:].bitcast(F32),
                           in_=bank[:].rearrange("p (a u) n -> p a n u", u=2))
            return grouped

        def quantise_w_in(w_grouped):
            codes = wgroup.tile([P, 2 * P], U32, tag="w_in_codes", align_bytes=64)
            scales = wgroup.tile([P, 2 * P], U8, tag="w_in_scales", align_bytes=64)
            nc.vector.quantize_mx(out=codes[:].bitcast(FP8X4), scales=scales[:],
                                  in_=w_grouped[:].rearrange("p a n j -> p (a n j)"))
            return codes, scales

        def multiply_x(codes, scales):
            xin_bank = psum_out.tile([P, P], F32, tag="out")
            for a in range(2):
                cols = slice(a * P, (a + 1) * P)
                nc.tensor.matmul_mx(out=xin_bank[:], lhsT=codes[:, cols].bitcast(FP8X4),
                                    lhsT_scale=scales[:, cols],
                                    rhs=x_codes[:, cols].bitcast(FP8X4), rhs_scale=x_scales[:, cols],
                                    start=(a == 0), stop=(a == 1))
            return xin_bank

        wo_codes = mxops.tile([P, 4, D], U32, align_bytes=64)
        wo_scales = mxops.tile([P, 4, D], U8, align_bytes=64)

        def group_w_out(bank):
            grouped = wgroup.tile([P, 2 * P, 4], BF16, tag="w_out_grouped", align_bytes=64)
            nc.scalar.copy(out=grouped[:].bitcast(F32), in_=bank[:].rearrange("p u r n -> p (r n) u"))
            return grouped

        def quantise_w_out(pair, c, grouped):
            rows_n = slice(pair * 2 * P, (pair + 1) * 2 * P)
            nc.vector.quantize_mx(out=wo_codes[:, c, rows_n].bitcast(FP8X4),
                                  scales=wo_scales[:, c, rows_n],
                                  in_=grouped[:].rearrange("p n j -> p (n j)"))

        def multiply_y(c, o_banks):
            for nb in range(2):
                rows_n = slice(nb * 512, (nb + 1) * 512)
                nc.tensor.matmul_mx(out=o_banks[nb][:],
                                    lhsT=y_codes[:, c * P : (c + 1) * P].bitcast(FP8X4),
                                    lhsT_scale=y_scales[:, c * P : (c + 1) * P],
                                    rhs=wo_codes[:, c, rows_n].bitcast(FP8X4),
                                    rhs_scale=wo_scales[:, c, rows_n],
                                    start=(c == 0), stop=(c == 3))

        y_grouped = mxops.tile([P, 4, P, 4], BF16, align_bytes=64)
        y_codes = mxops.tile([P, 4 * P], U32, align_bytes=64)
        y_scales = mxops.tile([P, 4 * P], U8, align_bytes=64)

        def turn_old_state(rows):
            banks = []
            for half_s in range(2):
                bank = psum_in.tile([P, 2, 2, P], F32, tag="in")
                for h in range(2):
                    words = rows[h][:].bitcast(F32).rearrange("t (f q) -> t q f", q=4)
                    for q in range(2):
                        nc.tensor.transpose(bank[:, h, q, :], words[:, 2 * half_s + q, :],
                                            ident_f32[:])
                banks.append(bank[:].bitcast(BF16).rearrange("p h q (t e) -> p h q e t", e=2))
            return banks

        def slot(old_t, s):
            return old_t[s // 4][:, :, s % 4 // 2, s % 2, :]

        def scale(k, old_t, slots=range(S)):
            if 0 in slots:
                sines[k] = work.tile([P, S, 2, P], F32, tag="sines", name="sines")
            for s in slots:
                one = slice(k * S + s, k * S + s + 1)
                for h, factor in enumerate((neg_sin_t, sin_t)):
                    nc.scalar.activation(out=sines[k][:, s, h, :], in_=slot(old_t, s)[:, 1 - h, :],
                                         func=ACT.Copy, scale=factor[:, one])

        def drive(k):
            sums = work.tile([P, S, 2, P], F32, tag="sums")
            for s in range(0, S, 4):
                b_slots = coefs[:, 1:3, k * S + s : k * S + s + 4].rearrange("p h s -> p s h")
                nc.gpsimd.tensor_tensor(
                    out=sums[:, s : s + 4, :, :],
                    in0=xin_t[:, k, :].unsqueeze(1).unsqueeze(1).to_broadcast([P, 4, 2, P]),
                    in1=b_slots.unsqueeze(3).to_broadcast([P, 4, 2, P]), op=ALU.mult)
            return sums

        def add_term(total, values, coefficient):
            nc.vector.scalar_tensor_tensor(out=total, in0=values, scalar=coefficient, in1=total,
                                           op0=ALU.mult, op1=ALU.add)

        def add_cosines(k, slots):
            for s in slots:
                add_term(sums[k][:, s, :, :], slot(old[k], s), cos_t[:, k * S + s : k * S + s + 1])

        def add_to_y(k, slots):
            old_t, y_part = old[k], y_parts[k]
            for s in slots:
                one = slice(k * S + s, k * S + s + 1)
                add_term(y_part[:, 0, :], slot(old_t, s)[:, 0, :], y_from_real_t[:, one])
                if s == 0:
                    nc.vector.tensor_scalar(out=y_part[:, 1, :], in0=slot(old_t, s)[:, 1, :],
                                            scalar1=y_from_imag_t[:, one], scalar2=None,
                                            op0=ALU.mult)
                else:
                    add_term(y_part[:, 1, :], slot(old_t, s)[:, 1, :], y_from_imag_t[:, one])

        def add_sines(k, h):
            nc.vector.tensor_tensor(out=sums[k][:, :, h, :], in0=sums[k][:, :, h, :],
                                    in1=sines[k][:, :, h, :], op=ALU.add)

        def rotate(k, slots):
            for s in slots:
                add_cosines(k, [s])
                add_to_y(k, [s])

        def turn_back(parts, new_rows, h, half_s, copy_out):
            back = psum_out.tile([P, 4, P], F32, tag="out")
            for j in range(4):
                s = half_s * 4 + j
                for n, part in enumerate(parts):
                    nc.tensor.matmul(back[:, j, :], lhsT=part[:, s, h, :], rhs=ident_f32[:],
                                     is_transpose=True, start=(n == 0), stop=(n == len(parts) - 1))
            copy_out(out=new_rows[:, :, half_s * 4 : (half_s + 1) * 4],
                     in_=back[:].rearrange("t j f -> t f j"))

        def store_state(k, h, new_rows):
            nc.sync.dma_start(out=state_out[h][:, k * COLS : (k + 1) * COLS],
                              in_=new_rows[:].rearrange("t f s -> t (f s)"))

        def round_y(k):
            y_back = psum_out.tile([P, P], F32, tag="out")
            for h in range(2):
                nc.tensor.matmul(y_back[:], lhsT=y_parts[k][:, h, :], rhs=ident_f32[:],
                                 is_transpose=True, start=(h == 0), stop=(h == 1))
            if k % 4 == 0:
                y_rows[k // 4] = small.tile([P, 512], BF16, name="y_rows")
            nc.scalar.copy(out=y_rows[k // 4][:, (k % 4) * P : (k % 4 + 1) * P], in_=y_back[:])

        def take_x_in(k):
            nc.scalar.copy(out=xin_t[:, k, :], in_=xin_bank[k][:])

        def start_y(k):
            y_parts[k] = small.tile([P, 2, P], F32, name="y_part", bufs=4)
            nc.gpsimd.tensor_scalar(out=y_parts[k][:, 0, :], in0=xin_t[:, k, :],
                                    scalar1=drive_y_t[:, k : k + 1], scalar2=0.0,
                                    op0=ALU.mult, op1=ALU.add)

        def group_y(c, y_rows):
            y_words = y_rows[:].bitcast(F32)
            y_bank = psum_out.tile([P, 2, P], F32, tag="out")
            for u in range(2):
                nc.tensor.transpose(y_bank[:, u, :], y_words[:, u : 256 : 2], ident_f32[:])
            nc.scalar.copy(out=y_grouped[:, c, :, :].bitcast(F32),
                           in_=y_bank[:].rearrange("p u t -> p t u"))

        def quantise_y(c):
            nc.vector.quantize_mx(out=y_codes[:, c * P : (c + 1) * P].bitcast(FP8X4),
                                  scales=y_scales[:, c * P : (c + 1) * P],
                                  in_=y_grouped[:, c, :, :].rearrange("p t q -> p (t q)"))

        xin_bank, old, sines, sums, y_parts, y_rows = {}, {}, {}, {}, {}, {}
        o_banks = []

        sin_touch = small.tile([P, 1], F32)
        nc.vector.memset(sin_touch[:], 0.0)
        root_touch = small.tile([P, 1], F32)
        nc.vector.memset(root_touch[:], 1.0)
        nc.scalar.activation(out=sin_touch[:], in_=sin_touch[:], func=ACT.Sin)
        n_coef = N_TILES * S
        coef_bank = psum_in.tile([P, S, P], BF16, tag="in")
        for s in range(S):
            nc.tensor.transpose(coef_bank[:, s, :], coef_rows[:, s : COLS : S], ident_bf16[:])
        coefs = tables.tile([P, 5, n_coef], F32)
        nc.scalar.copy(out=coefs[:].rearrange("p i (k s) -> p (i k) s", s=S),
                       in_=coef_bank[:, :, 0 : 5 * N_TILES].rearrange("p s j -> p j s"))
        theta = coefs[:, 0, :]
        b_t = [coefs[:, 1, :], coefs[:, 2, :]]
        c_t = [coefs[:, 3, :], coefs[:, 4, :]]
        x_bank = transpose_word_blocks(nc, psum_out, ident_f32, x_sb[:])
        x_grouped = mxops.tile([P, 2, P, 4], BF16, align_bytes=64)
        nc.scalar.copy(out=x_grouped[:].bitcast(F32),
                       in_=x_bank[:].rearrange("p (a u) n -> p a n u", u=2))
        w_grouped = group_words(transpose_word_blocks(nc, psum_out, ident_f32, w_in_rows[0][:]),
                                "w_in_grouped")
        old[0] = turn_old_state(rows[0])
        turns = tables.tile([P, n_coef], F32)
        nc.vector.tensor_scalar(out=turns[:], in0=theta, scalar1=1.0 / (2.0 * math.pi),
                                scalar2=ROUND_MAGIC, op0=ALU.mult, op1=ALU.add)
        nc.vector.tensor_scalar(out=turns[:], in0=turns[:], scalar1=ROUND_MAGIC, scalar2=None,
                                op0=ALU.subtract)
        reduced = tables.tile([P, n_coef], F32)
        nc.vector.scalar_tensor_tensor(out=reduced[:], in0=turns[:], scalar=-TWO_PI_HI,
                                       in1=theta, op0=ALU.mult, op1=ALU.add)
        nc.vector.scalar_tensor_tensor(out=reduced[:], in0=turns[:], scalar=-TWO_PI_MID,
                                       in1=reduced[:], op0=ALU.mult, op1=ALU.add)
        nc.vector.scalar_tensor_tensor(out=reduced[:], in0=turns[:], scalar=-TWO_PI_LO,
                                       in1=reduced[:], op0=ALU.mult, op1=ALU.add)
        nc.vector.tensor_scalar(out=reduced[:], in0=reduced[:], scalar1=PI_BELOW,
                                scalar2=-PI_BELOW, op0=ALU.min, op1=ALU.max)
        sin_t = tables.tile([P, n_coef], F32)
        nc.scalar.activation(out=sin_t[:], in_=reduced[:], func=ACT.Sin)
        half = tables.tile([P, n_coef], F32)
        nc.scalar.activation(out=half[:], in_=reduced[:], func=ACT.Sin, scale=0.5)
        nc.scalar.activation(out=half[:], in_=half[:], func=ACT.Square, scale=math.sqrt(2.0))
        nc.vector.quantize_mx(out=x_codes[:].bitcast(FP8X4), scales=x_scales[:],
                              in_=x_grouped[:].rearrange("p a n j -> p (a n j)"))

        xin_bank[0] = multiply_x(*quantise_w_in(w_grouped))
        take_x_in(0)
        sums[0] = drive(0)
        cos_t = tables.tile([P, n_coef], F32)
        nc.vector.tensor_scalar(out=cos_t[:], in0=half[:], scalar1=-1.0, scalar2=1.0,
                                op0=ALU.mult, op1=ALU.add)
        neg_sin_t = tables.tile([P, n_coef], F32)
        nc.vector.tensor_scalar(out=neg_sin_t[:], in0=sin_t[:], scalar1=-1.0, scalar2=None,
                                op0=ALU.mult)

        w_grouped = group_words(transpose_word_blocks(nc, psum_out, ident_f32, w_in_rows[1][:]),
                                "w_in_grouped")
        scale(0, old[0], range(4))

        def combine(name, first, first_sign, second, second_sign, with_first, with_second):
            part = tables.tile([P, n_coef], F32, tag="part", bufs=2)
            total = tables.tile([P, n_coef], F32, name=name)
            nc.vector.scalar_tensor_tensor(out=part[:], in0=first, scalar=first_sign,
                                           in1=with_first, op0=ALU.mult, op1=ALU.mult)
            nc.vector.scalar_tensor_tensor(out=total[:], in0=second, scalar=second_sign,
                                           in1=with_second, op0=ALU.mult, op1=ALU.mult)
            nc.vector.tensor_tensor(out=total[:], in0=total[:], in1=part[:], op=ALU.add)
            return total

        y_from_imag_t = combine("y_from_imag_t", c_t[0], -1.0, c_t[1], -1.0, sin_t[:], cos_t[:])
        y_from_real_t = combine("y_from_real_t", c_t[0], 1.0, c_t[1], -1.0, cos_t[:], sin_t[:])
        y_from_drive = combine("y_from_drive", c_t[0], 1.0, c_t[1], -1.0, b_t[0], b_t[1])
        drive_y_t = tables.tile([P, N_TILES], F32)
        nc.vector.tensor_reduce(out=drive_y_t[:],
                                in_=y_from_drive[:].rearrange("p (k s) -> p k s", s=S),
                                axis=AX.X, op=ALU.add)
        y_parts[0] = small.tile([P, 2, P], F32, name="y_part", bufs=4)
        nc.scalar.activation(out=y_parts[0][:, 0, :], in_=xin_t[:, 0, :], func=ACT.Copy,
                             scale=drive_y_t[:, 0:1])
        xin_bank[1] = multiply_x(*quantise_w_in(w_grouped))
        w_bank = transpose_word_blocks(nc, psum_out, ident_f32, w_in_rows[2][:])
        take_x_in(1)
        scale(0, old[0], range(4, 6))
        w_grouped = group_words(w_bank, "w_in_grouped")
        scale(0, old[0], range(6, S))
        nc.scalar.activation(out=root_touch[:], in_=root_touch[:], func=ACT.Abs_reciprocal_sqrt)
        rotate(0, range(3))
        old[1] = turn_old_state(rows[1])
        xin_bank[2] = multiply_x(*quantise_w_in(w_grouped))
        rotate(0, range(3, 4))
        w_bank = [transpose_word_blocks(nc, psum_out, ident_f32, w_in_rows[3][:]),
                  transpose_w_out_words(nc, psum_out, ident_f32, w_out_rows[0], 0)]

        k = N_TILES - 1
        for i in range(k):
            if i + 4 < N_TILES:
                rows[i + 4] = load_state(i + 4)
            if i + 5 < N_TILES:
                w_in_rows[i + 5] = load_w_in(i + 5)
            if i % 4 == 0 and i // 4 + 1 < 4:
                w_out_rows[i // 4 + 1] = load_w_out(i // 4 + 1)
            if i == 10:
                nc.sync.dma_start(out=norm_w_all[:], in_=norm_w.partition_broadcast(P))

            if i + 3 < N_TILES:
                w_grouped = group_words(w_bank[0], "w_in_grouped")
            wo_grouped = group_w_out(w_bank[1])
            if i + 2 < N_TILES:
                take_x_in(i + 2)
            if 1 <= i < N_TILES - 1:
                old[i + 1] = turn_old_state(rows[i + 1])
            if i >= 1:
                rotate(i, range(4))
            if i + 1 < N_TILES:
                scale(i + 1, old[i + 1])
            if i + 1 < N_TILES:
                start_y(i + 1)
                sums[i + 1] = drive(i + 1)
            if i >= 1:
                new_rows = leave.tile([P, P, S], F32, tag="new_rows0", name="new_rows0")
                for half_s in range(2):
                    turn_back((sines[i - 1], sums[i - 1]), new_rows, 0, half_s, nc.scalar.copy)
                store_state(i - 1, 0, new_rows)
                new_rows = leave.tile([P, P, S], F32, tag="new_rows1", name="new_rows1")
                turn_back((sines[i - 1], sums[i - 1]), new_rows, 1, 0, nc.scalar.copy)
            if i >= 1:
                turn_back((sines[i - 1], sums[i - 1]), new_rows, 1, 1, nc.scalar.copy)
                store_state(i - 1, 1, new_rows)
            rotate(i, range(4, 6))
            if i + 3 < N_TILES:
                w_quant = quantise_w_in(w_grouped)
            quantise_w_out(i // 4, i % 4, wo_grouped)
            if i >= 6 and i % 4 == 2:
                quantise_y(i // 4 - 1)
            rotate(i, range(6, S))
            if i >= 1:
                round_y(i - 1)
            if i >= 5 and i % 4 == 1:
                group_y(i // 4 - 1, y_rows[i // 4 - 1])
            if i + 4 < N_TILES:
                w_bank[0] = transpose_word_blocks(nc, psum_out, ident_f32, w_in_rows[i + 4][:])
            if i + 1 < N_TILES:
                w_bank[1] = transpose_w_out_words(nc, psum_out, ident_f32,
                                                  w_out_rows[(i + 1) // 4], (i + 1) % 4)
            if i + 3 < N_TILES:
                xin_bank[i + 3] = multiply_x(*w_quant)

        before_rows = [leave.tile([P, P, S], F32, tag="new_rows%d" % h, name="new_rows%d" % h)
                       for h in range(2)]
        wo_grouped = group_w_out(w_bank[1])
        add_to_y(k, range(S))
        add_cosines(k, range(2))
        quantise_w_out(3, 3, wo_grouped)
        add_cosines(k, range(2, S))
        for nb in range(2):
            o_bank = psum_in.tile([P, 512], F32, tag="in")
            o_banks.append(o_bank)
        turn_back((sines[k - 1], sums[k - 1]), before_rows[0], 0, 0, nc.scalar.copy)
        turn_back((sines[k - 1], sums[k - 1]), before_rows[0], 0, 1, nc.scalar.copy)
        store_state(k - 1, 0, before_rows[0])
        round_y(k - 1)
        multiply_y(0, o_banks)
        round_y(k)
        multiply_y(1, o_banks)
        group_y(3, y_rows[3])
        turn_back((sines[k - 1], sums[k - 1]), before_rows[1], 1, 0, nc.scalar.copy)
        quantise_y(3)
        turn_back((sines[k - 1], sums[k - 1]), before_rows[1], 1, 1, nc.vector.tensor_copy)
        store_state(k - 1, 1, before_rows[1])
        multiply_y(2, o_banks)
        multiply_y(3, o_banks)
        square_sums = small.tile([P, 2], F32)
        gained = mid.tile([P, D], F32)
        result = mid.tile([P, D], F32)
        squares = small.tile([P, 512], F32, tag="squares", name="squares")
        nc.scalar.activation(out=squares[:], in_=o_banks[0][:], func=ACT.Square,
                             accum_out=square_sums[:, 0:1])
        nc.vector.tensor_tensor(out=gained[:, 512:1024], in0=o_banks[1][:],
                                in1=norm_w_all[:, 512:1024], op=ALU.mult)
        squares = small.tile([P, 512], F32, tag="squares", name="squares")
        nc.scalar.activation(out=squares[:], in_=o_banks[1][:], func=ACT.Square,
                             accum_out=square_sums[:, 1:2])
        nc.vector.tensor_tensor(out=gained[:, 0:512], in0=o_banks[0][:],
                                in1=norm_w_all[:, 0:512], op=ALU.mult)
        total = small.tile([P, 1], F32)
        nc.vector.tensor_scalar(out=total[:], in0=square_sums[:, 0:1], scalar1=square_sums[:, 1:2],
                                scalar2=D * EPS, op0=ALU.add, op1=ALU.add)
        inv_rms = small.tile([P, 1], F32)
        nc.scalar.activation(out=inv_rms[:], in_=total[:], func=ACT.Abs_reciprocal_sqrt,
                             scale=1.0 / D)
        nc.vector.scalar_tensor_tensor(out=result[:, 0:512], in0=gained[:, 0:512],
                                       scalar=inv_rms[:, 0:1], in1=x_sb[:, 0:512],
                                       op0=ALU.mult, op1=ALU.add)
        nc.sync.dma_start(out=out_0.rearrange("b l d -> (b l) d")[:, 0:512],
                          in_=result[:, 0:512])
        nc.vector.scalar_tensor_tensor(out=result[:, 512:1024], in0=gained[:, 512:1024],
                                       scalar=inv_rms[:, 0:1], in1=x_sb[:, 512:1024],
                                       op0=ALU.mult, op1=ALU.add)
        nc.sync.dma_start(out=out_0.rearrange("b l d -> (b l) d")[:, 512:1024],
                          in_=result[:, 512:1024])
        last_rows = [leave.tile([P, P, S], F32, tag="new_rows%d" % h, name="new_rows%d" % h)
                     for h in range(2)]
        turn_back((sines[k], sums[k]), last_rows[0], 0, 0, nc.scalar.copy)
        turn_back((sines[k], sums[k]), last_rows[0], 0, 1, nc.scalar.copy)
        store_state(k, 0, last_rows[0])
        turn_back((sines[k], sums[k]), last_rows[1], 1, 0, nc.scalar.copy)
        turn_back((sines[k], sums[k]), last_rows[1], 1, 1, nc.vector.tensor_copy)
        store_state(k, 1, last_rows[1])
